import numpy as np
import ml_dtypes


def mxq(x, axis, fmt="e4m3"):
    dtype, down = {"e4m3": (ml_dtypes.float8_e4m3fn, 7), "e5m2": (ml_dtypes.float8_e5m2, 14)}[fmt]
    v = np.moveaxis(np.asarray(x, np.float32).astype(ml_dtypes.bfloat16).astype(np.float64), axis, -1)
    blocks = v.reshape(v.shape[:-1] + (-1, 32))
    amax = np.abs(blocks).max(-1, keepdims=True)
    byte = np.maximum(np.where(amax > 0, np.frexp(amax)[1] - 1 + 127, 0) - down, 1)
    scale = np.exp2(byte - 127.0)
    codes = (blocks / scale).astype(np.float32).astype(dtype).astype(np.float64)
    return np.moveaxis((codes * scale).reshape(v.shape), -1, axis)


WIDE = False


def mx_kscale(k):
    if not WIDE:
        return np.ones(k)
    levels = np.array([10, -10, 5, -5, 0])
    if k % 512:
        return np.exp2(np.random.permutation(np.resize(levels, k // 32))).repeat(32)
    a = np.empty((k // 512, 16))
    for p in range(k // 512):
        a[p, :8] = np.random.permutation(np.resize(levels, 8))
        for g in range(8):
            far = levels[np.abs(levels - a[p, g]) >= 10]
            a[p, g + 8] = far[np.random.randint(len(far))]
    return np.exp2(a.ravel()).repeat(32)


BF16 = ml_dtypes.bfloat16


def bf(x):
    return np.asarray(x, np.float32).astype(BF16)


def f64(x):
    return np.asarray(x).astype(np.float64)


B, I, O, DEG = 8192, 512, 128, 5
LN_EPS = 1e-5


def gottlieb_basis(x, alpha, degree):
    a = alpha[0]
    basis = [np.ones_like(x)]
    if degree >= 1:
        basis.append(2.0 * a * x)
    for n in range(2, degree + 1):
        basis.append(2.0 * (a + (n - 1)) * x * basis[-1] - (a + (2 * n - 2)) * basis[-2])
    return np.stack(basis, axis=0)


def setup_inputs():
    s = mx_kscale(I)
    u = s / s.max()
    p = u / (1.0 + np.exp(-np.random.standard_normal((B, I))))
    d = np.arange(DEG + 1)
    g = 0.5 ** d / np.sqrt(I * (DEG + 1))
    undo = np.where(d % 2 == 1, 1.0 / u[:, None, None], 1.0)
    return {"x": bf(np.log(p / (1.0 - p))),
            "alpha": bf(0.5 + 0.1 * np.random.standard_normal(1)),
            "coeffs": bf(np.random.standard_normal((I, O, DEG + 1)) * g * undo),
            "ln_weight": bf(1.0 + 0.1 * np.random.standard_normal(O)),
            "ln_bias": bf(0.1 * np.random.standard_normal(O))}


def reference(x, alpha, coeffs, ln_weight, ln_bias):
    xs = 1.0 / (1.0 + np.exp(-f64(x)))
    basis = gottlieb_basis(xs, f64(alpha), DEG)
    c = np.ascontiguousarray(f64(coeffs).transpose(2, 0, 1))
    y0 = c[0].sum(0)
    y = (mxq(basis[1:], 2, "e4m3") @ mxq(c[1:], 1, "e4m3")).sum(0) + y0
    mu = y.mean(-1, keepdims=True)
    var = np.square(y - mu).mean(-1, keepdims=True)
    y = (y - mu) / np.sqrt(var + LN_EPS)
    return y * f64(ln_weight) + f64(ln_bias)

@@ -1,0 +1,338 @@
+from contextlib import ExitStack
+
+import concourse.mybir as mybir
+from concourse.masks import make_identity
+
+F32 = mybir.dt.float32
+BF16 = mybir.dt.bfloat16
+U32 = mybir.dt.uint32
+U8 = mybir.dt.uint8
+FP8X4 = mybir.dt.float8_e4m3fn_x4
+ALU = mybir.AluOpType
+ACT = mybir.ActivationFunctionType
+
+P = 128
+B, I, O, DEG = 8192, 512, 128, 5
+NT = B // P
+G = 4
+SIZES = (2, 2) + (4,) * 14 + (2, 1, 1)
+NCH = len(SIZES)
+STARTS = tuple(sum(SIZES[:c]) for c in range(NCH))
+assert sum(SIZES) == NT
+CW = G * I
+NW = CW // 4
+LN_EPS = 1e-5
+FLOPS = 2 * B * I * O * DEG
+
+T1_VECTOR_COLS = tuple(g * I if c < 2 else 0 for c, g in enumerate(SIZES))
+
+
+def tile_gottliebkanlayer_t_kernel(tc, x, alpha, coeffs, ln_weight, ln_bias, out):
+    nc = tc.nc
+    x_v = x.rearrange("(p t) i -> p (t i)", t=NT)
+    out_v = out.rearrange("(p t) o -> p (t o)", t=NT)
+    with ExitStack() as ctx:
+        const = ctx.enter_context(tc.tile_pool(name="const", bufs=1))
+        xin = ctx.enter_context(tc.tile_pool(name="xin", bufs=4))
+        work = ctx.enter_context(tc.tile_pool(name="work", bufs=2))
+        small = ctx.enter_context(tc.tile_pool(name="small", bufs=3))
+        stat = ctx.enter_context(tc.tile_pool(name="stat", bufs=5))
+        psum = ctx.enter_context(tc.psum_pool(name="psum", bufs=2))
+        ctx.enter_context(tc.manual_schedule())
+
+        x_tiles = {}
+
+        def load_x(c):
+            x_sb = xin.tile([P, CW], BF16, name="x_sb")
+            nc.sync.dma_start(out=x_sb[:, 0:SIZES[c] * I], in_=x_v[:, STARTS[c] * I:(STARTS[c] + SIZES[c]) * I])
+            x_tiles[c] = x_sb
+
+        for c in range(4):
+            load_x(c)
+        a_bf = const.tile([P, 1], BF16, name="a_bf")
+        nc.scalar.dma_start(out=a_bf[:], in_=alpha.partition_broadcast(P))
+        craw = const.tile([P, 4 * O * 6], BF16, name="craw")
+        nc.scalar.dma_start(
+            out=craw[:], in_=coeffs.rearrange("(q t) o d -> q (t o d)", t=4),
+        )
+        g_b = const.tile([P, O], BF16, name="g_b")
+        nc.scalar.dma_start(out=g_b[:], in_=ln_weight.partition_broadcast(P))
+        b_b = const.tile([P, O], BF16, name="b_b")
+        nc.scalar.dma_start(out=b_b[:], in_=ln_bias.partition_broadcast(P))
+
+        cst0 = const.tile([P, 9], F32, name="cst0")
+        nc.vector.memset(cst0[:], 2.0)
+        for k, v in ((0, 0.0), (2, 6.0), (3, 1.0), (6, 3.0), (7, 4.0), (8, 8.0)):
+            nc.vector.memset(cst0[:, k:k + 1], v)
+        floors = const.tile([P, 3], F32, name="floors")
+        powe = const.tile([P, 3], F32, name="powe")
+        for k, (lo, ex) in enumerate(((1e-4, 0.5), (6e-3, 1.0), (5e-2, -0.5))):
+            nc.vector.memset(floors[:, k:k + 1], lo)
+            nc.vector.memset(powe[:, k:k + 1], ex)
+        mhalf = const.tile([P, G], F32, name="mhalf")
+        nc.vector.memset(mhalf[:], -0.5)
+        ones = const.tile([P, 64], BF16, name="ones")
+        nc.vector.memset(ones[:], 1.0)
+        ident = const.tile([P, P], F32, name="ident")
+        make_identity(nc, ident[:])
+
+        names = ("a0", "a2", "a6", "a1", "a2b", "a2c", "a3", "a4", "a8", "p01", "a2sq", "c40", "c42", "c31", "c33",
+                 "c44", "c55", "c51", "c53", "h3", "h4", "h5", "sg3", "sg4", "sg5", "aa3", "aa4", "aa5", "ab3", "ab4",
+                 "ab5", "r3", "r4", "r5", "v3", "t1", "u0", "u1", "w0", "w1", "m2", "e3", "x1", "b4", "yy", "k4", "mm",
+                 "m4", "t5", "b5", "nt", "e5", "s5", "c11", "c20")
+        sc = const.tile([P, len(names)], F32, name="sc")
+        idx = dict((n, k) for k, n in enumerate(names))
+
+        def col(n, w=1):
+            return sc[:, idx[n]:idx[n] + w]
+
+        def ts(o, i, s1, s2=None, op0=ALU.mult, op1=ALU.mult):
+            if s2 is None:
+                nc.vector.tensor_scalar(out=o, in0=i, scalar1=s1, scalar2=None, op0=op0)
+            else:
+                nc.vector.tensor_scalar(out=o, in0=i, scalar1=s1, scalar2=s2, op0=op0, op1=op1)
+
+        def stt(o, i0, s, i1, op0, op1):
+            nc.vector.scalar_tensor_tensor(out=o, in0=i0, scalar=s, in1=i1, op0=op0, op1=op1)
+
+        ts(col("a0", 9), cst0[:], a_bf[:, 0:1], op0=ALU.add)
+        nc.vector.tensor_tensor(out=col("p01", 3), in0=col("a0", 3), in1=col("a1", 3), op=ALU.mult)
+        stt(col("c33"), col("p01"), 8.0, col("a2"), ALU.mult, ALU.mult)
+        ts(col("c44"), col("c33"), col("a3"), 2.0)
+        ts(col("c55"), col("c44"), col("a4"), 2.0)
+        ts(col("h3", 3), col("c33", 3), 0.0, 0.5, ALU.is_ge, ALU.subtract)
+        stt(col("aa3", 3), col("c33", 3), 2.0, col("h3", 3), ALU.mult, ALU.mult)
+        nc.vector.tensor_tensor(out=col("ab3", 3), in0=col("aa3", 3), in1=floors[:], op=ALU.max)
+        gp = const.tile([P, 3], F32, name="gp")
+        nc.gpsimd.tensor_tensor(out=gp[:], in0=col("ab3", 3), in1=powe[:], op=ALU.pow)
+        s3 = gp[:, 0:1]
+        ir5 = gp[:, 2:3]
+        ts(col("c11"), col("a0"), 2.0)
+        ts(col("c20"), col("a2"), -1.0)
+        c20 = col("c20")
+        ts(col("sg3", 3), col("h3", 3), 2.0)
+        nc.vector.reciprocal(out=col("r3", 3), in_=col("ab3", 3))
+        ts(col("c31"), col("a2sq"), -4.0, 8.0, ALU.mult, ALU.add)
+        ts(col("v3"), col("p01"), col("a6"), -4.0)
+        ts(col("t1"), col("c31"), col("a3"), 2.0)
+        nc.vector.tensor_tensor(out=col("c42"), in0=col("t1"), in1=col("v3"), op=ALU.add)
+        ts(col("m2"), col("p01"), col("r3"), 4.0)
+        ts(col("e3"), col("c31"), col("sg3"))
+        ts(col("x1"), col("c42"), col("r4"), 0.5)
+        ts(col("b4"), col("x1"), col("ab3"), col("sg4"))
+        ts(col("u0", 2), col("c40", 2), col("a4"), 2.0)
+        ts(col("w0", 2), col("c31", 2), col("a8"))
+        nc.vector.tensor_tensor(out=col("c51", 2), in0=col("u0", 2), in1=col("w0", 2), op=ALU.subtract)
+        ts(col("t5"), col("c53"), ir5, 0.5)
+        ts(col("s5"), col("ab5"), ir5, col("r3"))
+        ts(col("b5"), col("t5"), col("sg5"))
+        ts(col("yy"), col("x1"), col("c42"), col("sg4"))
+        stt(col("k4"), col("yy"), -0.5, col("c40"), ALU.mult, ALU.add)
+        ts(col("mm"), col("r3"), col("r3"), col("ab4"))
+        ts(col("m4"), col("mm"), col("sg4"))
+        ts(col("nt"), col("t5"), col("t5"), -1.0)
+        stt(col("e5"), col("c51"), col("sg5"), col("nt"), ALU.mult, ALU.add)
+
+        xts = {}
+        zs = {}
+        w3s = {}
+        p4s = {}
+        p5s = {}
+        tbs = {}
+        cods = {}
+        scls = {}
+        yt_ps = {}
+        ytss = {}
+        ysts = {}
+        rstds = {}
+        ycgs = {}
+        mvs = {}
+        osbs = {}
+
+        def x_transposes(c):
+            xw = x_tiles[c][:].bitcast(F32)
+            for h in range((SIZES[c] + 1) // 2):
+                m = min(2, SIZES[c] - 2 * h)
+                xt = psum.tile([P, 512], F32, name="xt", tag="xt")
+                for j2 in range(m):
+                    for u in range(2):
+                        nc.tensor.transpose(
+                            xt[:, (u * m + j2) * P:(u * m + j2 + 1) * P],
+                            xw[:, (2 * h + j2) * 256 + u:(2 * h + j2 + 1) * 256:2],
+                            ident[:])
+                xts[(c, h)] = xt
+
+        def sigmoid(c):
+            z = work.tile([P, CW], F32, name="z")
+            for h in range((SIZES[c] + 1) // 2):
+                m = min(2, SIZES[c] - 2 * h)
+                nc.scalar.activation(
+                    out=z[:, h * 1024:h * 1024 + m * I].rearrange("p (n u e) -> p n u e", u=2, e=2),
+                    in_=xts[(c, h)][:].bitcast(BF16)[:, 0:4 * m * P].rearrange("p (u n e) -> p n u e", u=2, e=2),
+                    func=ACT.Sigmoid)
+            zs[c] = z
+
+        def square_w3(c):
+            w3 = work.tile([P, CW], F32, name="w3")
+            cw = SIZES[c] * I
+            nc.scalar.activation(out=w3[:, 0:cw], in_=zs[c][:, 0:cw], func=ACT.Square, scale=s3)
+            w3s[c] = w3
+
+        def squares_p4_p5(c):
+            w3 = w3s[c]
+            cw = SIZES[c] * I
+            p4 = work.tile([P, CW], F32, name="p4")
+            nc.scalar.activation(out=p4[:, 0:cw], in_=w3[:, 0:cw], func=ACT.Square, bias=col("b4"))
+            p5 = work.tile([P, CW], F32, name="p5")
+            nc.scalar.activation(out=p5[:, 0:cw], in_=w3[:, 0:cw], func=ACT.Square, scale=col("s5"), bias=col("b5"))
+            p4s[c], p5s[c] = p4, p5
+            tbs[c] = work.tile([P, DEG * CW], BF16, name="tb", align_bytes=64)
+
+        def t1_scalar(c):
+            cw, fc = SIZES[c] * I, T1_VECTOR_COLS[c]
+            if fc < cw:
+                nc.scalar.activation(out=tbs[c][:, fc:cw], in_=zs[c][:, fc:cw], func=ACT.Copy, scale=col("c11"))
+
+        def basis(c):
+            tb, z, w3 = tbs[c], zs[c], w3s[c]
+            cw, fc = SIZES[c] * I, T1_VECTOR_COLS[c]
+            ts(tb[:, cw:2 * cw], w3[:, 0:cw], col("m2"), c20, ALU.mult, ALU.add)
+            nc.vector.scalar_tensor_tensor(out=tb[:, 2 * cw:3 * cw], in0=w3[:, 0:cw], scalar=col("e3"), in1=z[:, 0:cw],
+                                           op0=ALU.add, op1=ALU.mult)
+            ts(tb[:, 3 * cw:4 * cw], p4s[c][:, 0:cw], col("m4"), col("k4"), ALU.mult, ALU.add)
+            nc.vector.scalar_tensor_tensor(out=tb[:, 4 * cw:5 * cw], in0=p5s[c][:, 0:cw], scalar=col("e5"),
+                                           in1=z[:, 0:cw], op0=ALU.add, op1=ALU.mult)
+            if fc > 0:
+                ts(tb[:, 0:fc], z[:, 0:fc], col("c11"))
+
+        def quantise(c):
+            cw, nw = SIZES[c] * I, SIZES[c] * P
+            cod = work.tile([P, DEG * NW], U32, name="cod", align_bytes=64)
+            scl = work.tile([P, DEG * NW], U8, name="scl", align_bytes=64)
+            for d0, d1 in ((2, 4), (4, 5), (0, 2)):
+                nc.vector.quantize_mx(out=cod[:, d0 * nw:d1 * nw].bitcast(FP8X4), scales=scl[:, d0 * nw:d1 * nw],
+                                      in_=tbs[c][:, d0 * cw:d1 * cw])
+            cods[c], scls[c] = cod, scl
+
+        def mx(c):
+            nw = SIZES[c] * P
+            yt = psum.tile([P, NW], F32, name="yt", tag="yt")
+            order = (2, 3, 4, 0, 1)
+            for n, d in enumerate(order):
+                nc.tensor.matmul_mx(
+                    out=yt[:, 0:nw],
+                    lhsT=ccod[:, d * O:(d + 1) * O].bitcast(FP8X4), lhsT_scale=cscl[:, d * O:(d + 1) * O],
+                    rhs=cods[c][:, d * nw:(d + 1) * nw].bitcast(FP8X4), rhs_scale=scls[c][:, d * nw:(d + 1) * nw],
+                    start=(n == 0), stop=(n == DEG - 1))
+            yt_ps[c] = yt
+
+        def evacuate(c):
+            yts = stat.tile([P, NW], F32, name="yts")
+            nw = SIZES[c] * P
+            nc.scalar.activation(out=yts[:, 0:nw], in_=yt_ps[c][:, 0:nw], func=ACT.Identity, bias=y0[:, 0:1])
+            ytss[c] = yts
+
+        def y_transposes(c):
+            yst = psum.tile([P, NW], F32, name="yst", tag="yst")
+            for j in range(SIZES[c]):
+                nc.tensor.transpose(yst[:, j * O:(j + 1) * O], ytss[c][:, j * P:(j + 1) * P], ident[:])
+            ysts[c] = yst
+
+        def stats(c):
+            st = stat.tile([P, G, 6], F32, name="st")
+            mv = stat.tile([P, G, 2], F32, name="mv")
+            for j in range(SIZES[c]):
+                nc.vector.bn_stats(out=st[:, j, :], in_=ysts[c][:, j * O:(j + 1) * O])
+            for j in range(SIZES[c]):
+                nc.vector.bn_aggr(out=mv[:, j, :], in_=st[:, j, :])
+            mvs[c] = mv
+
+        def rstd_of(c):
+            ve = stat.tile([P, G], F32, name="ve")
+            g = SIZES[c]
+            ts(ve[:, 0:g], mvs[c][:, 0:g, 1], LN_EPS, op0=ALU.add)
+            rstd = stat.tile([P, G], F32, name="rstd")
+            nc.gpsimd.tensor_tensor(out=rstd[:, 0:g], in0=ve[:, 0:g], in1=mhalf[:, 0:g], op=ALU.pow)
+            rstds[c] = rstd
+
+        def centre(c):
+            ycg = psum.tile([P, NW], F32, name="ycg", tag="ycg")
+            for j in range(SIZES[c]):
+                nc.tensor.matmul(out=ycg[:, j * O:(j + 1) * O], lhsT=ytss[c][:, j * P:(j + 1) * P], rhs=ceng[:],
+                                 start=True, stop=True)
+            ycgs[c] = ycg
+
+        def final(c, j0, j1):
+            if j0 == 0:
+                osbs[c] = small.tile([P, G * O], F32, name="osb")
+            osb = osbs[c]
+            for j in range(j0, j1):
+                nc.vector.scalar_tensor_tensor(out=osb[:, j * O:(j + 1) * O], in0=ycgs[c][:, j * O:(j + 1) * O],
+                                               scalar=rstds[c][:, j:j + 1], in1=b_b[:], op0=ALU.mult, op1=ALU.add)
+            if j1 == SIZES[c]:
+                nc.sync.dma_start(out=out_v[:, STARTS[c] * O:(STARTS[c] + SIZES[c]) * O], in_=osb[:, 0:SIZES[c] * O])
+
+        craw4 = craw[:].rearrange("p (t o d) -> p t o d", t=4, o=O, d=6)
+        c0 = const.tile([P, 4 * O], BF16, name="c0")
+        nc.gpsimd.tensor_scalar(out=c0[:].rearrange("p (t o) -> p t o", t=4), in0=craw4[:, :, :, 0],
+                                scalar1=1.0, scalar2=1.0, op0=ALU.mult, op1=ALU.mult)
+        cg = const.tile([P, DEG * 4 * O], BF16, name="cg", align_bytes=64)
+        for d in range(1, DEG + 1):
+            sign = {3: col("sg3"), 5: col("sg5")}.get(d, 1.0)
+            nc.gpsimd.tensor_scalar(
+                out=cg[:, (d - 1) * 4 * O:d * 4 * O].rearrange("p (o t) -> p o t", t=4),
+                in0=craw4[:, :, :, d].rearrange("p t o -> p o t"),
+                scalar1=sign, scalar2=1.0, op0=ALU.mult, op1=ALU.mult)
+        ccod = const.tile([P, DEG * O], U32, name="ccod", align_bytes=64)
+        cscl = const.tile([P, DEG * O], U8, name="cscl", align_bytes=64)
+        y0 = const.tile([P, 1], F32, name="y0")
+        cen = const.tile([P, O], F32, name="cen")
+        ceng = const.tile([P, O], F32, name="ceng")
+
+        def coefficient_work():
+            nc.vector.quantize_mx(out=ccod[:, 0:4 * O].bitcast(FP8X4), scales=cscl[:, 0:4 * O], in_=cg[:, 0:16 * O])
+            nc.vector.quantize_mx(out=ccod[:, 4 * O:5 * O].bitcast(FP8X4), scales=cscl[:, 4 * O:5 * O],
+                                  in_=cg[:, 16 * O:20 * O])
+            ps0 = psum.tile([P, 64], F32, name="ps0", tag="ycg")
+            for t in range(4):
+                nc.tensor.matmul(out=ps0[:], lhsT=c0[:, t * O:(t + 1) * O], rhs=ones[:], start=(t == 0),
+                                 stop=(t == 3))
+            nc.vector.tensor_copy(out=y0[:], in_=ps0[:, 0:1])
+            ts(cen[:], ident[:], -1.0 / O, op0=ALU.add)
+            nc.vector.tensor_tensor(out=ceng[:], in0=cen[:], in1=g_b[:], op=ALU.mult)
+
+        for c in range(2):
+            x_transposes(c)
+            sigmoid(c)
+        for k in range(NCH + 4):
+            if k < NCH:
+                square_w3(k)
+            if 0 <= k - 2 < NCH:
+                evacuate(k - 2)
+            if k < NCH:
+                squares_p4_p5(k)
+            if 1 <= k and k + 1 < NCH:
+                x_transposes(k + 1)
+            if k + 4 < NCH:
+                load_x(k + 4)
+            if 0 <= k - 2 < NCH:
+                y_transposes(k - 2)
+            if 0 <= k - 4:
+                centre(k - 4)
+            if 0 <= k - 1 < NCH:
+                mx(k - 1)
+            if 1 <= k and k + 1 < NCH:
+                sigmoid(k + 1)
+            if k < NCH:
+                t1_scalar(k)
+                basis(k)
+            if k == 0:
+                coefficient_work()
+            if 0 <= k - 3 < NCH:
+                rstd_of(k - 3)
+            if 0 <= k - 2 < NCH:
+                stats(k - 2)
+            if 0 <= k - 4:
+                final(k - 4, 0, SIZES[k - 4])
+            if k < NCH:
+                quantise(k)

@@ -14,17 +14,13 @@ ACT = mybir.ActivationFunctionType
 P = 128
 B, I, O, DEG = 8192, 512, 128, 5
 NT = B // P
-G = 4
-SIZES = (2, 2) + (4,) * 14 + (2, 1, 1)
-NCH = len(SIZES)
-STARTS = tuple(sum(SIZES[:c]) for c in range(NCH))
-assert sum(SIZES) == NT
+G = 2
+NCH = NT // G
 CW = G * I
-NW = CW // 4
+NW = G * P
 LN_EPS = 1e-5
 FLOPS = 2 * B * I * O * DEG
-
-T1_VECTOR_COLS = tuple(g * I if c < 2 else 0 for c, g in enumerate(SIZES))
+SLOT = {3: 0, 5: 1, 1: 2, 2: 3, 4: 4}
 
 
 def tile_gottliebkanlayer_t_kernel(tc, x, alpha, coeffs, ln_weight, ln_bias, out):
@@ -33,21 +29,22 @@ def tile_gottliebkanlayer_t_kernel(tc, x, alpha, coeffs, ln_weight, ln_bias, out
     out_v = out.rearrange("(p t) o -> p (t o)", t=NT)
     with ExitStack() as ctx:
         const = ctx.enter_context(tc.tile_pool(name="const", bufs=1))
-        xin = ctx.enter_context(tc.tile_pool(name="xin", bufs=4))
-        work = ctx.enter_context(tc.tile_pool(name="work", bufs=2))
-        small = ctx.enter_context(tc.tile_pool(name="small", bufs=3))
-        stat = ctx.enter_context(tc.tile_pool(name="stat", bufs=5))
-        psum = ctx.enter_context(tc.psum_pool(name="psum", bufs=2))
+        xin = ctx.enter_context(tc.tile_pool(name="xin", bufs=6))
+        work = ctx.enter_context(tc.tile_pool(name="work", bufs=3))
+        one = ctx.enter_context(tc.tile_pool(name="one", bufs=1))
+        stat = ctx.enter_context(tc.tile_pool(name="stat", bufs=6))
+        psz = ctx.enter_context(tc.psum_pool(name="psz", bufs=3 * G))
+        psy = ctx.enter_context(tc.psum_pool(name="psy", bufs=1))
         ctx.enter_context(tc.manual_schedule())
 
         x_tiles = {}
 
         def load_x(c):
             x_sb = xin.tile([P, CW], BF16, name="x_sb")
-            nc.sync.dma_start(out=x_sb[:, 0:SIZES[c] * I], in_=x_v[:, STARTS[c] * I:(STARTS[c] + SIZES[c]) * I])
+            nc.sync.dma_start(out=x_sb[:], in_=x_v[:, c * CW:(c + 1) * CW])
             x_tiles[c] = x_sb
 
-        for c in range(4):
+        for c in range(5):
             load_x(c)
         a_bf = const.tile([P, 1], BF16, name="a_bf")
         nc.scalar.dma_start(out=a_bf[:], in_=alpha.partition_broadcast(P))
@@ -133,144 +130,141 @@ def tile_gottliebkanlayer_t_kernel(tc, x, alpha, coeffs, ln_weight, ln_bias, out
         ts(col("nt"), col("t5"), col("t5"), -1.0)
         stt(col("e5"), col("c51"), col("sg5"), col("nt"), ALU.mult, ALU.add)
 
-        xts = {}
-        zs = {}
+        zns = {}
+        zps = {}
         w3s = {}
         p4s = {}
         p5s = {}
-        tbs = {}
+        t35s = {}
+        t1s = {}
+        t24s = {}
         cods = {}
         scls = {}
-        yt_ps = {}
-        ytss = {}
-        ysts = {}
-        rstds = {}
-        ycgs = {}
+        yts = {}
+        ysbs = {}
+        yys = {}
         mvs = {}
-        osbs = {}
+        ves = {}
+        rstds = {}
 
-        def x_transposes(c):
-            xw = x_tiles[c][:].bitcast(F32)
-            for h in range((SIZES[c] + 1) // 2):
-                m = min(2, SIZES[c] - 2 * h)
-                xt = psum.tile([P, 512], F32, name="xt", tag="xt")
-                for j2 in range(m):
-                    for u in range(2):
-                        nc.tensor.transpose(
-                            xt[:, (u * m + j2) * P:(u * m + j2 + 1) * P],
-                            xw[:, (2 * h + j2) * 256 + u:(2 * h + j2 + 1) * 256:2],
-                            ident[:])
-                xts[(c, h)] = xt
+        def by_row(ap):
+            return ap.rearrange("p (t n) -> p n t", t=4)
+
+        def sub(tile, r):
+            return tile[:, r * I:(r + 1) * I].rearrange("p (n t) -> p n t", t=4)
 
         def sigmoid(c):
-            z = work.tile([P, CW], F32, name="z")
-            for h in range((SIZES[c] + 1) // 2):
-                m = min(2, SIZES[c] - 2 * h)
-                nc.scalar.activation(
-                    out=z[:, h * 1024:h * 1024 + m * I].rearrange("p (n u e) -> p n u e", u=2, e=2),
-                    in_=xts[(c, h)][:].bitcast(BF16)[:, 0:4 * m * P].rearrange("p (u n e) -> p n u e", u=2, e=2),
-                    func=ACT.Sigmoid)
-            zs[c] = z
+            zn = work.tile([P, CW], F32, name="zn")
+            nc.scalar.activation(out=zn[:].rearrange("p (r t q) -> p r t q", r=G, t=4),
+                                 in_=x_tiles[c][:].rearrange("p (r q t) -> p r t q", r=G, t=4), func=ACT.Sigmoid)
+            zns[c] = zn
+
+        def z_transposes(c):
+            for r in range(G):
+                zp = psz.tile([P, I], F32, name="zp")
+                for t in range(4):
+                    nc.tensor.transpose(zp[:, t * P:(t + 1) * P], zns[c][:, (r * 4 + t) * P:(r * 4 + t + 1) * P], ident[:])
+                zps[(c, r)] = zp
 
         def square_w3(c):
             w3 = work.tile([P, CW], F32, name="w3")
-            cw = SIZES[c] * I
-            nc.scalar.activation(out=w3[:, 0:cw], in_=zs[c][:, 0:cw], func=ACT.Square, scale=s3)
+            for r in range(G):
+                nc.scalar.activation(out=sub(w3, r), in_=by_row(zps[(c, r)][:]), func=ACT.Square, scale=s3)
             w3s[c] = w3
 
-        def squares_p4_p5(c):
-            w3 = w3s[c]
-            cw = SIZES[c] * I
+        def square_p4(c):
             p4 = work.tile([P, CW], F32, name="p4")
-            nc.scalar.activation(out=p4[:, 0:cw], in_=w3[:, 0:cw], func=ACT.Square, bias=col("b4"))
+            nc.scalar.activation(out=p4[:], in_=w3s[c][:], func=ACT.Square, bias=col("b4"))
+            p4s[c] = p4
+
+        def square_p5(c):
             p5 = work.tile([P, CW], F32, name="p5")
-            nc.scalar.activation(out=p5[:, 0:cw], in_=w3[:, 0:cw], func=ACT.Square, scale=col("s5"), bias=col("b5"))
-            p4s[c], p5s[c] = p4, p5
-            tbs[c] = work.tile([P, DEG * CW], BF16, name="tb", align_bytes=64)
+            nc.scalar.activation(out=p5[:], in_=w3s[c][:], func=ACT.Square, scale=col("s5"), bias=col("b5"))
+            p5s[c] = p5
 
         def t1_scalar(c):
-            cw, fc = SIZES[c] * I, T1_VECTOR_COLS[c]
-            if fc < cw:
-                nc.scalar.activation(out=tbs[c][:, fc:cw], in_=zs[c][:, fc:cw], func=ACT.Copy, scale=col("c11"))
+            t1s[c] = work.tile([P, CW], BF16, name="t1", align_bytes=64)
+            nc.scalar.activation(out=sub(t1s[c], 0), in_=by_row(zps[(c, 0)][:]), func=ACT.Copy, scale=col("c11"))
 
-        def basis(c):
-            tb, z, w3 = tbs[c], zs[c], w3s[c]
-            cw, fc = SIZES[c] * I, T1_VECTOR_COLS[c]
-            ts(tb[:, cw:2 * cw], w3[:, 0:cw], col("m2"), c20, ALU.mult, ALU.add)
-            nc.vector.scalar_tensor_tensor(out=tb[:, 2 * cw:3 * cw], in0=w3[:, 0:cw], scalar=col("e3"), in1=z[:, 0:cw],
+        def t1_vector(c):
+            ts(sub(t1s[c], 1), by_row(zps[(c, 1)][:]), col("c11"))
+
+        def t3_t5(c, d, r):
+            if (d, r) == (3, 0):
+                t35s[c] = work.tile([P, 2 * CW], BF16, name="t35", align_bytes=64)
+            src, add = {3: (w3s[c], col("e3")), 5: (p5s[c], col("e5"))}[d]
+            half = t35s[c][:, (0 if d == 3 else CW):(CW if d == 3 else 2 * CW)]
+            nc.vector.scalar_tensor_tensor(out=sub(half, r), in0=sub(src, r), scalar=add, in1=by_row(zps[(c, r)][:]),
                                            op0=ALU.add, op1=ALU.mult)
-            ts(tb[:, 3 * cw:4 * cw], p4s[c][:, 0:cw], col("m4"), col("k4"), ALU.mult, ALU.add)
-            nc.vector.scalar_tensor_tensor(out=tb[:, 4 * cw:5 * cw], in0=p5s[c][:, 0:cw], scalar=col("e5"),
-                                           in1=z[:, 0:cw], op0=ALU.add, op1=ALU.mult)
-            if fc > 0:
-                ts(tb[:, 0:fc], z[:, 0:fc], col("c11"))
 
-        def quantise(c):
-            cw, nw = SIZES[c] * I, SIZES[c] * P
-            cod = work.tile([P, DEG * NW], U32, name="cod", align_bytes=64)
-            scl = work.tile([P, DEG * NW], U8, name="scl", align_bytes=64)
-            for d0, d1 in ((2, 4), (4, 5), (0, 2)):
-                nc.vector.quantize_mx(out=cod[:, d0 * nw:d1 * nw].bitcast(FP8X4), scales=scl[:, d0 * nw:d1 * nw],
-                                      in_=tbs[c][:, d0 * cw:d1 * cw])
-            cods[c], scls[c] = cod, scl
+        def t2_gpsimd(c):
+            t24s[c] = one.tile([P, 2 * CW], BF16, name="t24", align_bytes=64)
+            nc.gpsimd.tensor_scalar(out=t24s[c][:, 0:CW], in0=w3s[c][:], scalar1=col("m2"), scalar2=c20, op0=ALU.mult,
+                                    op1=ALU.add)
+
+        def t4_gpsimd(c):
+            nc.gpsimd.tensor_scalar(out=t24s[c][:, CW:2 * CW], in0=p4s[c][:], scalar1=col("m4"), scalar2=col("k4"),
+                                    op0=ALU.mult, op1=ALU.add)
+
+        def quantise(c, src, d0, d1):
+            if d0 == 3:
+                cods[c] = work.tile([P, DEG * NW], U32, name="cod", align_bytes=64)
+                scls[c] = work.tile([P, DEG * NW], U8, name="scl", align_bytes=64)
+            cols = slice(SLOT[d0] * NW, (SLOT[d1] + 1) * NW)
+            nc.vector.quantize_mx(out=cods[c][:, cols].bitcast(FP8X4), scales=scls[c][:, cols], in_=src[:])
 
         def mx(c):
-            nw = SIZES[c] * P
-            yt = psum.tile([P, NW], F32, name="yt", tag="yt")
-            order = (2, 3, 4, 0, 1)
-            for n, d in enumerate(order):
+            yt = psy.tile([P, NW], F32, name="yt")
+            for n, d in enumerate((3, 5, 1, 2, 4)):
+                cols = slice(SLOT[d] * NW, (SLOT[d] + 1) * NW)
                 nc.tensor.matmul_mx(
-                    out=yt[:, 0:nw],
-                    lhsT=ccod[:, d * O:(d + 1) * O].bitcast(FP8X4), lhsT_scale=cscl[:, d * O:(d + 1) * O],
-                    rhs=cods[c][:, d * nw:(d + 1) * nw].bitcast(FP8X4), rhs_scale=scls[c][:, d * nw:(d + 1) * nw],
+                    out=yt[:],
+                    lhsT=ccod[:, (d - 1) * O:d * O].bitcast(FP8X4), lhsT_scale=cscl[:, (d - 1) * O:d * O],
+                    rhs=cods[c][:, cols].bitcast(FP8X4), rhs_scale=scls[c][:, cols],
                     start=(n == 0), stop=(n == DEG - 1))
-            yt_ps[c] = yt
+            yts[c] = yt
 
         def evacuate(c):
-            yts = stat.tile([P, NW], F32, name="yts")
-            nw = SIZES[c] * P
-            nc.scalar.activation(out=yts[:, 0:nw], in_=yt_ps[c][:, 0:nw], func=ACT.Identity, bias=y0[:, 0:1])
-            ytss[c] = yts
+            ysb = stat.tile([P, NW], F32, name="ysb")
+            nc.scalar.activation(out=ysb[:], in_=yts[c][:], func=ACT.Identity, bias=y0[:, 0:1])
+            ysbs[c] = ysb
 
-        def y_transposes(c):
-            yst = psum.tile([P, NW], F32, name="yst", tag="yst")
-            for j in range(SIZES[c]):
-                nc.tensor.transpose(yst[:, j * O:(j + 1) * O], ytss[c][:, j * P:(j + 1) * P], ident[:])
-            ysts[c] = yst
+        def y_transposes(c, yy):
+            for j in range(G):
+                nc.tensor.transpose(yy[:, j * O:(j + 1) * O], ysbs[c][:, j * P:(j + 1) * P], ident[:])
 
-        def stats(c):
-            st = stat.tile([P, G, 6], F32, name="st")
-            mv = stat.tile([P, G, 2], F32, name="mv")
-            for j in range(SIZES[c]):
-                nc.vector.bn_stats(out=st[:, j, :], in_=ysts[c][:, j * O:(j + 1) * O])
-            for j in range(SIZES[c]):
-                nc.vector.bn_aggr(out=mv[:, j, :], in_=st[:, j, :])
-            mvs[c] = mv
+        def centre(c, yy):
+            for j in range(G):
+                nc.tensor.matmul(out=yy[:, (G + j) * O:(G + j + 1) * O], lhsT=ysbs[c][:, j * P:(j + 1) * P], rhs=ceng[:],
+                                 start=True, stop=True)
+
+        def stats(c, yy, j):
+            if j == 0:
+                mvs[c] = (stat.tile([P, G, 6], F32, name="st"), stat.tile([P, G, 2], F32, name="mv"))
+            nc.vector.bn_stats(out=mvs[c][0][:, j, :], in_=yy[:, j * O:(j + 1) * O])
+
+        def aggregate(c, j):
+            nc.vector.bn_aggr(out=mvs[c][1][:, j, :], in_=mvs[c][0][:, j, :])
+
+        def add_eps(c):
+            ve = stat.tile([P, G], F32, name="ve")
+            ts(ve[:], mvs[c][1][:, :, 1], LN_EPS, op0=ALU.add)
+            ves[c] = ve
 
         def rstd_of(c):
-            ve = stat.tile([P, G], F32, name="ve")
-            g = SIZES[c]
-            ts(ve[:, 0:g], mvs[c][:, 0:g, 1], LN_EPS, op0=ALU.add)
             rstd = stat.tile([P, G], F32, name="rstd")
-            nc.gpsimd.tensor_tensor(out=rstd[:, 0:g], in0=ve[:, 0:g], in1=mhalf[:, 0:g], op=ALU.pow)
+            nc.gpsimd.tensor_tensor(out=rstd[:], in0=ves[c][:], in1=mhalf[:], op=ALU.pow)
             rstds[c] = rstd
 
-        def centre(c):
-            ycg = psum.tile([P, NW], F32, name="ycg", tag="ycg")
-            for j in range(SIZES[c]):
-                nc.tensor.matmul(out=ycg[:, j * O:(j + 1) * O], lhsT=ytss[c][:, j * P:(j + 1) * P], rhs=ceng[:],
-                                 start=True, stop=True)
-            ycgs[c] = ycg
+        osbs = {}
 
-        def final(c, j0, j1):
-            if j0 == 0:
-                osbs[c] = small.tile([P, G * O], F32, name="osb")
-            osb = osbs[c]
-            for j in range(j0, j1):
-                nc.vector.scalar_tensor_tensor(out=osb[:, j * O:(j + 1) * O], in0=ycgs[c][:, j * O:(j + 1) * O],
-                                               scalar=rstds[c][:, j:j + 1], in1=b_b[:], op0=ALU.mult, op1=ALU.add)
-            if j1 == SIZES[c]:
-                nc.sync.dma_start(out=out_v[:, STARTS[c] * O:(STARTS[c] + SIZES[c]) * O], in_=osb[:, 0:SIZES[c] * O])
+        def final(c, yy, j):
+            if j == 0:
+                osbs[c] = stat.tile([P, G * O], F32, name="osb")
+            nc.vector.scalar_tensor_tensor(out=osbs[c][:, j * O:(j + 1) * O], in0=yy[:, (G + j) * O:(G + j + 1) * O],
+                                           scalar=rstds[c][:, j:j + 1], in1=b_b[:], op0=ALU.mult, op1=ALU.add)
+            if j == G - 1:
+                nc.sync.dma_start(out=out_v[:, c * G * O:(c + 1) * G * O], in_=osbs[c][:])
 
         craw4 = craw[:].rearrange("p (t o d) -> p t o d", t=4, o=O, d=6)
         c0 = const.tile([P, 4 * O], BF16, name="c0")
@@ -293,7 +287,7 @@ def tile_gottliebkanlayer_t_kernel(tc, x, alpha, coeffs, ln_weight, ln_bias, out
             nc.vector.quantize_mx(out=ccod[:, 0:4 * O].bitcast(FP8X4), scales=cscl[:, 0:4 * O], in_=cg[:, 0:16 * O])
             nc.vector.quantize_mx(out=ccod[:, 4 * O:5 * O].bitcast(FP8X4), scales=cscl[:, 4 * O:5 * O],
                                   in_=cg[:, 16 * O:20 * O])
-            ps0 = psum.tile([P, 64], F32, name="ps0", tag="ycg")
+            ps0 = psy.tile([P, 64], F32, name="ps0", tag="yt")
             for t in range(4):
                 nc.tensor.matmul(out=ps0[:], lhsT=c0[:, t * O:(t + 1) * O], rhs=ones[:], start=(t == 0),
                                  stop=(t == 3))
@@ -301,38 +295,64 @@ def tile_gottliebkanlayer_t_kernel(tc, x, alpha, coeffs, ln_weight, ln_bias, out
             ts(cen[:], ident[:], -1.0 / O, op0=ALU.add)
             nc.vector.tensor_tensor(out=ceng[:], in0=cen[:], in1=g_b[:], op=ALU.mult)
 
-        for c in range(2):
-            x_transposes(c)
-            sigmoid(c)
-        for k in range(NCH + 4):
-            if k < NCH:
+        sigmoid(0)
+        sigmoid(1)
+        z_transposes(0)
+
+        def live(c):
+            return 0 <= c < NCH
+
+        for k in range(NCH + 5):
+            if live(k - 2):
+                mx(k - 2)
+            if live(k):
                 square_w3(k)
-            if 0 <= k - 2 < NCH:
+            if live(k + 1):
+                z_transposes(k + 1)
+            if live(k - 2):
                 evacuate(k - 2)
-            if k < NCH:
-                squares_p4_p5(k)
-            if 1 <= k and k + 1 < NCH:
-                x_transposes(k + 1)
-            if k + 4 < NCH:
-                load_x(k + 4)
-            if 0 <= k - 2 < NCH:
-                y_transposes(k - 2)
-            if 0 <= k - 4:
-                centre(k - 4)
-            if 0 <= k - 1 < NCH:
-                mx(k - 1)
-            if 1 <= k and k + 1 < NCH:
-                sigmoid(k + 1)
-            if k < NCH:
+            if live(k):
+                square_p4(k)
+            yy = yys.get(k - 1)
+            for j in range(G):
+                if live(k - 5):
+                    final(k - 5, yy, j)
+                if live(k - 3):
+                    stats(k - 3, yy, j)
+            if live(k - 2) or live(k - 4):
+                yys[k] = psy.tile([P, 2 * G * O], F32, name="yy")
+                if live(k - 2):
+                    y_transposes(k - 2, yys[k])
+                if live(k - 4):
+                    centre(k - 4, yys[k])
+            if live(k + 2):
+                sigmoid(k + 2)
+            if live(k + 5):
+                load_x(k + 5)
+            if live(k):
+                square_p5(k)
                 t1_scalar(k)
-                basis(k)
-            if k == 0:
+            if live(k - 1):
+                t2_gpsimd(k - 1)
+            if live(k - 4):
+                rstd_of(k - 4)
+            if live(k - 1):
+                t4_gpsimd(k - 1)
+            for r in range(G):
+                if live(k - 1):
+                    t3_t5(k - 1, 3, r)
+                if live(k - 3):
+                    aggregate(k - 3, r)
+            if live(k - 1):
+                t3_t5(k - 1, 5, 0)
+                t3_t5(k - 1, 5, 1)
+                t1_vector(k - 1)
+            if k == 1:
                 coefficient_work()
-            if 0 <= k - 3 < NCH:
-                rstd_of(k - 3)
-            if 0 <= k - 2 < NCH:
-                stats(k - 2)
-            if 0 <= k - 4:
-                final(k - 4, 0, SIZES[k - 4])
-            if k < NCH:
-                quantise(k)
+            if live(k - 1):
+                quantise(k - 1, t35s[k - 1], 3, 5)
+            if live(k - 3):
+                add_eps(k - 3)
+            if live(k - 1):
+                quantise(k - 1, t1s[k - 1], 1, 1)
+                quantise(k - 1, t24s[k - 1], 2, 4)

@@ -20,7 +20,7 @@ CW = G * I
 NW = G * P
 LN_EPS = 1e-5
 FLOPS = 2 * B * I * O * DEG
-SLOT = {3: 0, 5: 1, 1: 2, 2: 3, 4: 4}
+SLOT = {1: 0, 2: 1, 3: 2, 4: 3, 5: 4}
 
 
 def tile_gottliebkanlayer_t_kernel(tc, x, alpha, coeffs, ln_weight, ln_bias, out):
@@ -44,18 +44,18 @@ def tile_gottliebkanlayer_t_kernel(tc, x, alpha, coeffs, ln_weight, ln_bias, out
             nc.sync.dma_start(out=x_sb[:], in_=x_v[:, c * CW:(c + 1) * CW])
             x_tiles[c] = x_sb
 
-        for c in range(5):
-            load_x(c)
         a_bf = const.tile([P, 1], BF16, name="a_bf")
-        nc.scalar.dma_start(out=a_bf[:], in_=alpha.partition_broadcast(P))
+        nc.sync.dma_start(out=a_bf[:], in_=alpha.partition_broadcast(P))
+        load_x(0)
+        load_x(1)
         craw = const.tile([P, 4 * O * 6], BF16, name="craw")
-        nc.scalar.dma_start(
-            out=craw[:], in_=coeffs.rearrange("(q t) o d -> q (t o d)", t=4),
-        )
+        nc.sync.dma_start(out=craw[:], in_=coeffs.rearrange("(q t) o d -> q (t o d)", t=4))
+        for c in range(2, 5):
+            load_x(c)
         g_b = const.tile([P, O], BF16, name="g_b")
-        nc.scalar.dma_start(out=g_b[:], in_=ln_weight.partition_broadcast(P))
+        nc.sync.dma_start(out=g_b[:], in_=ln_weight.partition_broadcast(P))
         b_b = const.tile([P, O], BF16, name="b_b")
-        nc.scalar.dma_start(out=b_b[:], in_=ln_bias.partition_broadcast(P))
+        nc.sync.dma_start(out=b_b[:], in_=ln_bias.partition_broadcast(P))
 
         cst0 = const.tile([P, 9], F32, name="cst0")
         nc.vector.memset(cst0[:], 2.0)
@@ -135,15 +135,14 @@ def tile_gottliebkanlayer_t_kernel(tc, x, alpha, coeffs, ln_weight, ln_bias, out
         w3s = {}
         p4s = {}
         p5s = {}
-        t35s = {}
+        tbs = {}
         t1s = {}
-        t24s = {}
         cods = {}
         scls = {}
         yts = {}
         ysbs = {}
         yys = {}
-        mvs = {}
+        sts = {}
         ves = {}
         rstds = {}
 
@@ -190,24 +189,21 @@ def tile_gottliebkanlayer_t_kernel(tc, x, alpha, coeffs, ln_weight, ln_bias, out
             ts(sub(t1s[c], 1), by_row(zps[(c, 1)][:]), col("c11"))
 
         def t3_t5(c, d, r):
-            if (d, r) == (3, 0):
-                t35s[c] = work.tile([P, 2 * CW], BF16, name="t35", align_bytes=64)
             src, add = {3: (w3s[c], col("e3")), 5: (p5s[c], col("e5"))}[d]
-            half = t35s[c][:, (0 if d == 3 else CW):(CW if d == 3 else 2 * CW)]
-            nc.vector.scalar_tensor_tensor(out=sub(half, r), in0=sub(src, r), scalar=add, in1=by_row(zps[(c, r)][:]),
+            nc.vector.scalar_tensor_tensor(out=sub(tbs[c][:, (d - 2) * CW:(d - 1) * CW], r), in0=sub(src, r), scalar=add, in1=by_row(zps[(c, r)][:]),
                                            op0=ALU.add, op1=ALU.mult)
 
         def t2_gpsimd(c):
-            t24s[c] = one.tile([P, 2 * CW], BF16, name="t24", align_bytes=64)
-            nc.gpsimd.tensor_scalar(out=t24s[c][:, 0:CW], in0=w3s[c][:], scalar1=col("m2"), scalar2=c20, op0=ALU.mult,
+            tbs[c] = one.tile([P, 4 * CW], BF16, name="tb", align_bytes=64)
+            nc.gpsimd.tensor_scalar(out=tbs[c][:, 0:CW], in0=w3s[c][:], scalar1=col("m2"), scalar2=c20, op0=ALU.mult,
                                     op1=ALU.add)
 
         def t4_gpsimd(c):
-            nc.gpsimd.tensor_scalar(out=t24s[c][:, CW:2 * CW], in0=p4s[c][:], scalar1=col("m4"), scalar2=col("k4"),
+            nc.gpsimd.tensor_scalar(out=tbs[c][:, 2 * CW:3 * CW], in0=p4s[c][:], scalar1=col("m4"), scalar2=col("k4"),
                                     op0=ALU.mult, op1=ALU.add)
 
         def quantise(c, src, d0, d1):
-            if d0 == 3:
+            if d0 == 1:
                 cods[c] = work.tile([P, DEG * NW], U32, name="cod", align_bytes=64)
                 scls[c] = work.tile([P, DEG * NW], U8, name="scl", align_bytes=64)
             cols = slice(SLOT[d0] * NW, (SLOT[d1] + 1) * NW)
@@ -215,7 +211,7 @@ def tile_gottliebkanlayer_t_kernel(tc, x, alpha, coeffs, ln_weight, ln_bias, out
 
         def mx(c):
             yt = psy.tile([P, NW], F32, name="yt")
-            for n, d in enumerate((3, 5, 1, 2, 4)):
+            for n, d in enumerate((1, 2, 3, 4, 5)):
                 cols = slice(SLOT[d] * NW, (SLOT[d] + 1) * NW)
                 nc.tensor.matmul_mx(
                     out=yt[:],
@@ -233,22 +229,20 @@ def tile_gottliebkanlayer_t_kernel(tc, x, alpha, coeffs, ln_weight, ln_bias, out
             for j in range(G):
                 nc.tensor.transpose(yy[:, j * O:(j + 1) * O], ysbs[c][:, j * P:(j + 1) * P], ident[:])
 
-        def centre(c, yy):
+        def centre(c, yy, first):
             for j in range(G):
-                nc.tensor.matmul(out=yy[:, (G + j) * O:(G + j + 1) * O], lhsT=ysbs[c][:, j * P:(j + 1) * P], rhs=ceng[:],
+                nc.tensor.matmul(out=yy[:, (first + j) * O:(first + j + 1) * O], lhsT=ysbs[c][:, j * P:(j + 1) * P], rhs=ceng[:],
                                  start=True, stop=True)
 
-        def stats(c, yy, j):
-            if j == 0:
-                mvs[c] = (stat.tile([P, G, 6], F32, name="st"), stat.tile([P, G, 2], F32, name="mv"))
-            nc.vector.bn_stats(out=mvs[c][0][:, j, :], in_=yy[:, j * O:(j + 1) * O])
-
-        def aggregate(c, j):
-            nc.vector.bn_aggr(out=mvs[c][1][:, j, :], in_=mvs[c][0][:, j, :])
+        def stats(c, yy):
+            st = stat.tile([P, G, 3], F32, name="st")
+            nc.vector.bn_stats(out=st[:].rearrange("p j s -> p (j s)"),
+                               in_=yy[:, 0:G * O].rearrange("p (j o) -> p o j", j=G))
+            sts[c] = st
 
         def add_eps(c):
             ve = stat.tile([P, G], F32, name="ve")
-            ts(ve[:], mvs[c][1][:, :, 1], LN_EPS, op0=ALU.add)
+            ts(ve[:], sts[c][:, :, 2], 1.0 / O, LN_EPS, ALU.mult, ALU.add)
             ves[c] = ve
 
         def rstd_of(c):
@@ -258,25 +252,29 @@ def tile_gottliebkanlayer_t_kernel(tc, x, alpha, coeffs, ln_weight, ln_bias, out
 
         osbs = {}
 
-        def final(c, yy, j):
+        def final(c, yy, first, j):
             if j == 0:
                 osbs[c] = stat.tile([P, G * O], F32, name="osb")
-            nc.vector.scalar_tensor_tensor(out=osbs[c][:, j * O:(j + 1) * O], in0=yy[:, (G + j) * O:(G + j + 1) * O],
+            nc.vector.scalar_tensor_tensor(out=osbs[c][:, j * O:(j + 1) * O], in0=yy[:, (first + j) * O:(first + j + 1) * O],
                                            scalar=rstds[c][:, j:j + 1], in1=b_b[:], op0=ALU.mult, op1=ALU.add)
             if j == G - 1:
                 nc.sync.dma_start(out=out_v[:, c * G * O:(c + 1) * G * O], in_=osbs[c][:])
 
         craw4 = craw[:].rearrange("p (t o d) -> p t o d", t=4, o=O, d=6)
-        c0 = const.tile([P, 4 * O], BF16, name="c0")
-        nc.gpsimd.tensor_scalar(out=c0[:].rearrange("p (t o) -> p t o", t=4), in0=craw4[:, :, :, 0],
-                                scalar1=1.0, scalar2=1.0, op0=ALU.mult, op1=ALU.mult)
         cg = const.tile([P, DEG * 4 * O], BF16, name="cg", align_bytes=64)
-        for d in range(1, DEG + 1):
+
+        def regroup(eng, d):
             sign = {3: col("sg3"), 5: col("sg5")}.get(d, 1.0)
-            nc.gpsimd.tensor_scalar(
+            eng.tensor_scalar(
                 out=cg[:, (d - 1) * 4 * O:d * 4 * O].rearrange("p (o t) -> p o t", t=4),
                 in0=craw4[:, :, :, d].rearrange("p t o -> p o t"),
                 scalar1=sign, scalar2=1.0, op0=ALU.mult, op1=ALU.mult)
+
+        regroup(nc.gpsimd, 4)
+        regroup(nc.gpsimd, 3)
+        regroup(nc.gpsimd, 5)
+        regroup(nc.vector, 1)
+        regroup(nc.vector, 2)
         ccod = const.tile([P, DEG * O], U32, name="ccod", align_bytes=64)
         cscl = const.tile([P, DEG * O], U8, name="cscl", align_bytes=64)
         y0 = const.tile([P, 1], F32, name="y0")
@@ -289,7 +287,7 @@ def tile_gottliebkanlayer_t_kernel(tc, x, alpha, coeffs, ln_weight, ln_bias, out
                                   in_=cg[:, 16 * O:20 * O])
             ps0 = psy.tile([P, 64], F32, name="ps0", tag="yt")
             for t in range(4):
-                nc.tensor.matmul(out=ps0[:], lhsT=c0[:, t * O:(t + 1) * O], rhs=ones[:], start=(t == 0),
+                nc.tensor.matmul(out=ps0[:], lhsT=craw4[:, t, :, 0], rhs=ones[:], start=(t == 0),
                                  stop=(t == 3))
             nc.vector.tensor_copy(out=y0[:], in_=ps0[:, 0:1])
             ts(cen[:], ident[:], -1.0 / O, op0=ALU.add)
@@ -302,36 +300,31 @@ def tile_gottliebkanlayer_t_kernel(tc, x, alpha, coeffs, ln_weight, ln_bias, out
         def live(c):
             return 0 <= c < NCH
 
-        for k in range(NCH + 5):
+        for k in range(NCH):
             if live(k - 2):
                 mx(k - 2)
-            if live(k):
-                square_w3(k)
+            square_w3(k)
+            t1_scalar(k)
             if live(k + 1):
                 z_transposes(k + 1)
             if live(k - 2):
                 evacuate(k - 2)
-            if live(k):
-                square_p4(k)
-            yy = yys.get(k - 1)
+            square_p4(k)
             for j in range(G):
                 if live(k - 5):
-                    final(k - 5, yy, j)
-                if live(k - 3):
-                    stats(k - 3, yy, j)
-            if live(k - 2) or live(k - 4):
+                    final(k - 5, yys[k - 1], G, j)
+            if live(k - 3):
+                stats(k - 3, yys[k - 1])
+            if live(k - 2):
                 yys[k] = psy.tile([P, 2 * G * O], F32, name="yy")
-                if live(k - 2):
-                    y_transposes(k - 2, yys[k])
+                y_transposes(k - 2, yys[k])
                 if live(k - 4):
-                    centre(k - 4, yys[k])
+                    centre(k - 4, yys[k], G)
             if live(k + 2):
                 sigmoid(k + 2)
             if live(k + 5):
                 load_x(k + 5)
-            if live(k):
-                square_p5(k)
-                t1_scalar(k)
+            square_p5(k)
             if live(k - 1):
                 t2_gpsimd(k - 1)
             if live(k - 4):
@@ -341,8 +334,6 @@ def tile_gottliebkanlayer_t_kernel(tc, x, alpha, coeffs, ln_weight, ln_bias, out
             for r in range(G):
                 if live(k - 1):
                     t3_t5(k - 1, 3, r)
-                if live(k - 3):
-                    aggregate(k - 3, r)
             if live(k - 1):
                 t3_t5(k - 1, 5, 0)
                 t3_t5(k - 1, 5, 1)
@@ -350,9 +341,52 @@ def tile_gottliebkanlayer_t_kernel(tc, x, alpha, coeffs, ln_weight, ln_bias, out
             if k == 1:
                 coefficient_work()
             if live(k - 1):
-                quantise(k - 1, t35s[k - 1], 3, 5)
+                quantise(k - 1, t1s[k - 1], 1, 1)
             if live(k - 3):
                 add_eps(k - 3)
             if live(k - 1):
-                quantise(k - 1, t1s[k - 1], 1, 1)
-                quantise(k - 1, t24s[k - 1], 2, 4)
+                quantise(k - 1, tbs[k - 1], 2, 5)
+
+        L = NCH - 1
+        mx(L - 1)
+        evacuate(L - 1)
+        for j in range(G):
+            final(L - 4, yys[L], G, j)
+        stats(L - 2, yys[L])
+        late = psy.tile([P, 2 * G * O], F32, name="yy")
+        centre(L - 3, late, 0)
+        centre(L - 2, late, G)
+        own1 = psz.tile([P, I], F32, name="zp")
+        y_transposes(L - 1, own1)
+        centre(L - 1, own1, G)
+        t2_gpsimd(L)
+        rstd_of(L - 3)
+        t4_gpsimd(L)
+        for r in range(G):
+            t3_t5(L, 3, r)
+        for r in range(G):
+            t3_t5(L, 5, r)
+        t1_vector(L)
+        stats(L - 1, own1)
+        quantise(L, t1s[L], 1, 1)
+        add_eps(L - 2)
+        add_eps(L - 1)
+        quantise(L, tbs[L], 2, 5)
+        rstd_of(L - 2)
+        rstd_of(L - 1)
+        mx(L)
+        evacuate(L)
+        own0 = psz.tile([P, I], F32, name="zp")
+        y_transposes(L, own0)
+        centre(L, own0, G)
+        for j in range(G):
+            final(L - 3, late, 0, j)
+        for j in range(G):
+            final(L - 2, late, G, j)
+        for j in range(G):
+            final(L - 1, own1, G, j)
+        stats(L, own0)
+        add_eps(L)
+        rstd_of(L)
+        for j in range(G):
+            final(L, own0, G, j)

@@ -18,9 +18,16 @@ G = 2
 NCH = NT // G
 CW = G * I
 NW = G * P
+GMAX = 4
+SIZES = (GMAX,) * 15 + (2, 1, 1)
+NG = len(SIZES)
+FIRST = tuple(sum(SIZES[:g]) for g in range(NG))
+GROUP_OF = tuple(g for g in range(NG) for n in range(SIZES[g]))
+T1_FIRST = tuple(min(FIRST[GROUP_OF[q]], NT - 2) for q in range(NT))
+assert sum(SIZES) == NT
+T1_SCALAR_ROWS = (1, 0) * (NCH // 2 - 2) + (1,) + (2,) * 3
 LN_EPS = 1e-5
 FLOPS = 2 * B * I * O * DEG
-SLOT = {1: 0, 2: 1, 3: 2, 4: 3, 5: 4}
 
 
 def tile_gottliebkanlayer_t_kernel(tc, x, alpha, coeffs, ln_weight, ln_bias, out):
@@ -31,8 +38,9 @@ def tile_gottliebkanlayer_t_kernel(tc, x, alpha, coeffs, ln_weight, ln_bias, out
         const = ctx.enter_context(tc.tile_pool(name="const", bufs=1))
         xin = ctx.enter_context(tc.tile_pool(name="xin", bufs=6))
         work = ctx.enter_context(tc.tile_pool(name="work", bufs=3))
+        ahead = ctx.enter_context(tc.tile_pool(name="ahead", bufs=3))
         one = ctx.enter_context(tc.tile_pool(name="one", bufs=1))
-        stat = ctx.enter_context(tc.tile_pool(name="stat", bufs=6))
+        stat = ctx.enter_context(tc.tile_pool(name="stat", bufs=8))
         psz = ctx.enter_context(tc.psum_pool(name="psz", bufs=3 * G))
         psy = ctx.enter_context(tc.psum_pool(name="psy", bufs=1))
         ctx.enter_context(tc.manual_schedule())
@@ -50,7 +58,7 @@ def tile_gottliebkanlayer_t_kernel(tc, x, alpha, coeffs, ln_weight, ln_bias, out
         load_x(1)
         craw = const.tile([P, 4 * O * 6], BF16, name="craw")
         nc.sync.dma_start(out=craw[:], in_=coeffs.rearrange("(q t) o d -> q (t o d)", t=4))
-        for c in range(2, 5):
+        for c in range(2, 6):
             load_x(c)
         g_b = const.tile([P, O], BF16, name="g_b")
         nc.sync.dma_start(out=g_b[:], in_=ln_weight.partition_broadcast(P))
@@ -62,11 +70,12 @@ def tile_gottliebkanlayer_t_kernel(tc, x, alpha, coeffs, ln_weight, ln_bias, out
         for k, v in ((0, 0.0), (2, 6.0), (3, 1.0), (6, 3.0), (7, 4.0), (8, 8.0)):
             nc.vector.memset(cst0[:, k:k + 1], v)
         floors = const.tile([P, 3], F32, name="floors")
-        powe = const.tile([P, 3], F32, name="powe")
-        for k, (lo, ex) in enumerate(((1e-4, 0.5), (6e-3, 1.0), (5e-2, -0.5))):
+        powe = const.tile([P, 2], F32, name="powe")
+        for k, lo in enumerate((1e-4, 6e-3, 5e-2)):
             nc.vector.memset(floors[:, k:k + 1], lo)
+        for k, ex in enumerate((0.5, -0.5)):
             nc.vector.memset(powe[:, k:k + 1], ex)
-        mhalf = const.tile([P, G], F32, name="mhalf")
+        mhalf = const.tile([P, 2 * G], F32, name="mhalf")
         nc.vector.memset(mhalf[:], -0.5)
         ones = const.tile([P, 64], BF16, name="ones")
         nc.vector.memset(ones[:], 1.0)
@@ -95,18 +104,22 @@ def tile_gottliebkanlayer_t_kernel(tc, x, alpha, coeffs, ln_weight, ln_bias, out
         ts(col("a0", 9), cst0[:], a_bf[:, 0:1], op0=ALU.add)
         nc.vector.tensor_tensor(out=col("p01", 3), in0=col("a0", 3), in1=col("a1", 3), op=ALU.mult)
         stt(col("c33"), col("p01"), 8.0, col("a2"), ALU.mult, ALU.mult)
-        ts(col("c44"), col("c33"), col("a3"), 2.0)
-        ts(col("c55"), col("c44"), col("a4"), 2.0)
-        ts(col("h3", 3), col("c33", 3), 0.0, 0.5, ALU.is_ge, ALU.subtract)
-        stt(col("aa3", 3), col("c33", 3), 2.0, col("h3", 3), ALU.mult, ALU.mult)
-        nc.vector.tensor_tensor(out=col("ab3", 3), in0=col("aa3", 3), in1=floors[:], op=ALU.max)
-        gp = const.tile([P, 3], F32, name="gp")
-        nc.gpsimd.tensor_tensor(out=gp[:], in0=col("ab3", 3), in1=powe[:], op=ALU.pow)
+        gp = const.tile([P, 2], F32, name="gp")
         s3 = gp[:, 0:1]
-        ir5 = gp[:, 2:3]
+        ir5 = gp[:, 1:2]
+        ts(col("h3"), col("c33"), 0.0, 0.5, ALU.is_ge, ALU.subtract)
+        stt(col("aa3"), col("c33"), 2.0, col("h3"), ALU.mult, ALU.mult)
+        nc.vector.tensor_tensor(out=col("ab3"), in0=col("aa3"), in1=floors[:, 0:1], op=ALU.max)
+        nc.gpsimd.tensor_tensor(out=s3, in0=col("ab3"), in1=powe[:, 0:1], op=ALU.pow)
+        ts(col("c44"), col("c33"), col("a3"), 2.0)
         ts(col("c11"), col("a0"), 2.0)
+        ts(col("c55"), col("c44"), col("a4"), 2.0)
         ts(col("c20"), col("a2"), -1.0)
         c20 = col("c20")
+        ts(col("h4", 2), col("c44", 2), 0.0, 0.5, ALU.is_ge, ALU.subtract)
+        stt(col("aa4", 2), col("c44", 2), 2.0, col("h4", 2), ALU.mult, ALU.mult)
+        nc.vector.tensor_tensor(out=col("ab4", 2), in0=col("aa4", 2), in1=floors[:, 1:3], op=ALU.max)
+        nc.gpsimd.tensor_tensor(out=ir5, in0=col("ab5"), in1=powe[:, 1:2], op=ALU.pow)
         ts(col("sg3", 3), col("h3", 3), 2.0)
         nc.vector.reciprocal(out=col("r3", 3), in_=col("ab3", 3))
         ts(col("c31"), col("a2sq"), -4.0, 8.0, ALU.mult, ALU.add)
@@ -135,10 +148,10 @@ def tile_gottliebkanlayer_t_kernel(tc, x, alpha, coeffs, ln_weight, ln_bias, out
         w3s = {}
         p4s = {}
         p5s = {}
-        tbs = {}
+        odds = {}
+        evens = {}
         t1s = {}
-        cods = {}
-        scls = {}
+        codes = {}
         yts = {}
         ysbs = {}
         yys = {}
@@ -146,14 +159,29 @@ def tile_gottliebkanlayer_t_kernel(tc, x, alpha, coeffs, ln_weight, ln_bias, out
         ves = {}
         rstds = {}
 
+        def both(c):
+            return range(G * c, G * (c + 1))
+
+        def columns(qs):
+            first = FIRST[GROUP_OF[qs.start]]
+            return slice((qs.start - first) * I, (qs.stop - first) * I)
+
         def by_row(ap):
             return ap.rearrange("p (t n) -> p n t", t=4)
 
-        def sub(tile, r):
-            return tile[:, r * I:(r + 1) * I].rearrange("p (n t) -> p n t", t=4)
+        def rows_of(ap):
+            return ap.rearrange("p (n t) -> p n t", t=4)
+
+        def one_row(q):
+            return columns(range(q, q + 1))
+
+        def group_tile(tiles, g, name):
+            if g not in tiles:
+                tiles[g] = work.tile([P, GMAX * I], F32, name=name)
+            return tiles[g]
 
         def sigmoid(c):
-            zn = work.tile([P, CW], F32, name="zn")
+            zn = ahead.tile([P, CW], F32, name="zn")
             nc.scalar.activation(out=zn[:].rearrange("p (r t q) -> p r t q", r=G, t=4),
                                  in_=x_tiles[c][:].rearrange("p (r q t) -> p r t q", r=G, t=4), func=ACT.Sigmoid)
             zns[c] = zn
@@ -163,67 +191,112 @@ def tile_gottliebkanlayer_t_kernel(tc, x, alpha, coeffs, ln_weight, ln_bias, out
                 zp = psz.tile([P, I], F32, name="zp")
                 for t in range(4):
                     nc.tensor.transpose(zp[:, t * P:(t + 1) * P], zns[c][:, (r * 4 + t) * P:(r * 4 + t + 1) * P], ident[:])
-                zps[(c, r)] = zp
+                zps[G * c + r] = zp
 
-        def square_w3(c):
-            w3 = work.tile([P, CW], F32, name="w3")
-            for r in range(G):
-                nc.scalar.activation(out=sub(w3, r), in_=by_row(zps[(c, r)][:]), func=ACT.Square, scale=s3)
-            w3s[c] = w3
+        def square_w3(qs):
+            w3 = group_tile(w3s, GROUP_OF[qs.start], "w3")
+            for q in reversed(qs):
+                nc.scalar.activation(out=rows_of(w3[:, one_row(q)]), in_=by_row(zps[q][:]), func=ACT.Square, scale=s3)
 
-        def square_p4(c):
-            p4 = work.tile([P, CW], F32, name="p4")
-            nc.scalar.activation(out=p4[:], in_=w3s[c][:], func=ACT.Square, bias=col("b4"))
-            p4s[c] = p4
+        def square_p4(qs):
+            g, cols = GROUP_OF[qs.start], columns(qs)
+            nc.scalar.activation(out=group_tile(p4s, g, "p4")[:, cols], in_=w3s[g][:, cols], func=ACT.Square,
+                                 bias=col("b4"))
 
-        def square_p5(c):
-            p5 = work.tile([P, CW], F32, name="p5")
-            nc.scalar.activation(out=p5[:], in_=w3s[c][:], func=ACT.Square, scale=col("s5"), bias=col("b5"))
-            p5s[c] = p5
+        def square_p5(qs):
+            g, cols = GROUP_OF[qs.start], columns(qs)
+            nc.scalar.activation(out=group_tile(p5s, g, "p5")[:, cols], in_=w3s[g][:, cols], func=ACT.Square,
+                                 scale=col("s5"), bias=col("b5"))
+
+        def t1_out(q):
+            first = T1_FIRST[q]
+            if first not in t1s:
+                t1s[first] = work.tile([P, GMAX * I], BF16, name="t1", align_bytes=64)
+            return rows_of(t1s[first][:, (q - first) * I:(q - first + 1) * I])
 
         def t1_scalar(c):
-            t1s[c] = work.tile([P, CW], BF16, name="t1", align_bytes=64)
-            nc.scalar.activation(out=sub(t1s[c], 0), in_=by_row(zps[(c, 0)][:]), func=ACT.Copy, scale=col("c11"))
+            for q in both(c)[:T1_SCALAR_ROWS[c]]:
+                nc.scalar.activation(out=t1_out(q), in_=by_row(zps[q][:]), func=ACT.Copy, scale=col("c11"))
 
         def t1_vector(c):
-            ts(sub(t1s[c], 1), by_row(zps[(c, 1)][:]), col("c11"))
+            for q in both(c)[T1_SCALAR_ROWS[c]:]:
+                ts(t1_out(q), by_row(zps[q][:]), col("c11"))
 
-        def t3_t5(c, d, r):
-            src, add = {3: (w3s[c], col("e3")), 5: (p5s[c], col("e5"))}[d]
-            nc.vector.scalar_tensor_tensor(out=sub(tbs[c][:, (d - 2) * CW:(d - 1) * CW], r), in0=sub(src, r), scalar=add, in1=by_row(zps[(c, r)][:]),
+        def new_odd(g):
+            odds[g] = work.tile([P, 2 * GMAX * I], BF16, name="odd", align_bytes=64)
+
+        def new_even(g, pool, name):
+            evens[g] = pool.tile([P, 2 * GMAX * I], BF16, name=name, align_bytes=64)
+
+        def t3_t5(q, d):
+            g = GROUP_OF[q]
+            src, add = {3: (w3s[g], col("e3")), 5: (p5s[g], col("e5"))}[d]
+            cols = one_row(q)
+            shift = SIZES[g] * I if d == 5 else 0
+            nc.vector.scalar_tensor_tensor(out=rows_of(odds[g][:, shift + cols.start:shift + cols.stop]),
+                                           in0=rows_of(src[:, cols]), scalar=add, in1=by_row(zps[q][:]),
                                            op0=ALU.add, op1=ALU.mult)
 
-        def t2_gpsimd(c):
-            tbs[c] = one.tile([P, 4 * CW], BF16, name="tb", align_bytes=64)
-            nc.gpsimd.tensor_scalar(out=tbs[c][:, 0:CW], in0=w3s[c][:], scalar1=col("m2"), scalar2=c20, op0=ALU.mult,
-                                    op1=ALU.add)
-
-        def t4_gpsimd(c):
-            nc.gpsimd.tensor_scalar(out=tbs[c][:, 2 * CW:3 * CW], in0=p4s[c][:], scalar1=col("m4"), scalar2=col("k4"),
+        def t2_gpsimd(g):
+            w = SIZES[g] * I
+            nc.gpsimd.tensor_scalar(out=evens[g][:, 0:w], in0=w3s[g][:, 0:w], scalar1=col("m2"), scalar2=c20,
                                     op0=ALU.mult, op1=ALU.add)
 
-        def quantise(c, src, d0, d1):
-            if d0 == 1:
-                cods[c] = work.tile([P, DEG * NW], U32, name="cod", align_bytes=64)
-                scls[c] = work.tile([P, DEG * NW], U8, name="scl", align_bytes=64)
-            cols = slice(SLOT[d0] * NW, (SLOT[d1] + 1) * NW)
-            nc.vector.quantize_mx(out=cods[c][:, cols].bitcast(FP8X4), scales=scls[c][:, cols], in_=src[:])
+        def t4_gpsimd(g):
+            w = SIZES[g] * I
+            nc.gpsimd.tensor_scalar(out=evens[g][:, w:2 * w], in0=p4s[g][:, 0:w], scalar1=col("m4"), scalar2=col("k4"),
+                                    op0=ALU.mult, op1=ALU.add)
 
-        def mx(c):
-            yt = psy.tile([P, NW], F32, name="yt")
-            for n, d in enumerate((1, 2, 3, 4, 5)):
-                cols = slice(SLOT[d] * NW, (SLOT[d] + 1) * NW)
+        def vector_odd(qs):
+            for q in reversed(qs):
+                t3_t5(q, 5)
+            if len(qs) == G:
+                t1_vector(qs.start // G)
+            for q in reversed(qs):
+                t3_t5(q, 3)
+
+        def quantised(src, width):
+            cod = work.tile([P, width // 4], U32, name="cod%d" % width, align_bytes=64)
+            scl = work.tile([P, width // 4], U8, name="scl%d" % width, align_bytes=64)
+            nc.vector.quantize_mx(out=cod[:].bitcast(FP8X4), scales=scl[:], in_=src[:, 0:width])
+            return cod, scl
+
+        def quantise_t1(qs):
+            cod, scl = quantised(t1s[qs.start], len(qs) * I)
+            for q in qs:
+                codes[(q, 1)] = (cod, scl, (q - qs.start) * P)
+
+        def quantise_pair(g, tiles, degrees):
+            size = SIZES[g]
+            cod, scl = quantised(tiles[g], 2 * size * I)
+            for h, d in enumerate(degrees):
+                for q in range(FIRST[g], FIRST[g] + size):
+                    codes[(q, d)] = (cod, scl, (h * size + q - FIRST[g]) * P)
+
+        def quantise_odd(g):
+            quantise_pair(g, odds, (3, 5))
+
+        def quantise_even(g):
+            quantise_pair(g, evens, (2, 4))
+
+        def mx(qs, yt):
+            for n, d in enumerate((1, 3, 5, 2, 4)):
+                cod, scl, first = codes[(qs.start, d)]
+                cols = slice(first, first + len(qs) * P)
                 nc.tensor.matmul_mx(
-                    out=yt[:],
+                    out=yt[:, 0:len(qs) * P],
                     lhsT=ccod[:, (d - 1) * O:d * O].bitcast(FP8X4), lhsT_scale=cscl[:, (d - 1) * O:d * O],
-                    rhs=cods[c][:, cols].bitcast(FP8X4), rhs_scale=scls[c][:, cols],
+                    rhs=cod[:, cols].bitcast(FP8X4), rhs_scale=scl[:, cols],
                     start=(n == 0), stop=(n == DEG - 1))
-            yts[c] = yt
+            yts[qs.start] = yt
 
-        def evacuate(c):
-            ysb = stat.tile([P, NW], F32, name="ysb")
-            nc.scalar.activation(out=ysb[:], in_=yts[c][:], func=ACT.Identity, bias=y0[:, 0:1])
-            ysbs[c] = ysb
+        def evacuate(qs):
+            c = qs.start // G
+            if c not in ysbs:
+                ysbs[c] = stat.tile([P, NW], F32, name="ysb")
+            j = qs.start - G * c
+            nc.scalar.activation(out=ysbs[c][:, j * P:(j + len(qs)) * P], in_=yts[qs.start][:, 0:len(qs) * P],
+                                 func=ACT.Identity, bias=y0[:, 0:1])
 
         def y_transposes(c, yy):
             for j in range(G):
@@ -231,34 +304,32 @@ def tile_gottliebkanlayer_t_kernel(tc, x, alpha, coeffs, ln_weight, ln_bias, out
 
         def centre(c, yy, first):
             for j in range(G):
-                nc.tensor.matmul(out=yy[:, (first + j) * O:(first + j + 1) * O], lhsT=ysbs[c][:, j * P:(j + 1) * P], rhs=ceng[:],
-                                 start=True, stop=True)
+                nc.tensor.matmul(out=yy[:, (first + j) * O:(first + j + 1) * O], lhsT=ysbs[c][:, j * P:(j + 1) * P],
+                                 rhs=ceng[:], start=True, stop=True)
 
         def stats(c, yy):
-            st = stat.tile([P, G, 3], F32, name="st")
-            nc.vector.bn_stats(out=st[:].rearrange("p j s -> p (j s)"),
+            m, h = divmod(c, 2)
+            if h == 0:
+                sts[m] = stat.tile([P, 2 * G, 3], F32, name="st")
+                ves[m] = stat.tile([P, 2 * G], F32, name="ve")
+                rstds[m] = stat.tile([P, 2 * G], F32, name="rstd")
+            nc.vector.bn_stats(out=sts[m][:, h * G:(h + 1) * G, :].rearrange("p j s -> p (j s)"),
                                in_=yy[:, 0:G * O].rearrange("p (j o) -> p o j", j=G))
-            sts[c] = st
 
-        def add_eps(c):
-            ve = stat.tile([P, G], F32, name="ve")
-            ts(ve[:], sts[c][:, :, 2], 1.0 / O, LN_EPS, ALU.mult, ALU.add)
-            ves[c] = ve
+        def add_eps(m, h0=0, h1=2):
+            ts(ves[m][:, h0 * G:h1 * G], sts[m][:, h0 * G:h1 * G, 2], 1.0 / O, LN_EPS, ALU.mult, ALU.add)
 
-        def rstd_of(c):
-            rstd = stat.tile([P, G], F32, name="rstd")
-            nc.gpsimd.tensor_tensor(out=rstd[:], in0=ves[c][:], in1=mhalf[:], op=ALU.pow)
-            rstds[c] = rstd
+        def rstd_of(m, h0=0, h1=2):
+            cols = slice(h0 * G, h1 * G)
+            nc.gpsimd.tensor_tensor(out=rstds[m][:, cols], in0=ves[m][:, cols], in1=mhalf[:, cols], op=ALU.pow)
 
-        osbs = {}
-
-        def final(c, yy, first, j):
-            if j == 0:
-                osbs[c] = stat.tile([P, G * O], F32, name="osb")
-            nc.vector.scalar_tensor_tensor(out=osbs[c][:, j * O:(j + 1) * O], in0=yy[:, (first + j) * O:(first + j + 1) * O],
-                                           scalar=rstds[c][:, j:j + 1], in1=b_b[:], op0=ALU.mult, op1=ALU.add)
-            if j == G - 1:
-                nc.sync.dma_start(out=out_v[:, c * G * O:(c + 1) * G * O], in_=osbs[c][:])
+        def final(c, yy, first):
+            osb = stat.tile([P, G * O], F32, name="osb")
+            for j in range(G):
+                k = (c % 2) * G + j
+                nc.vector.scalar_tensor_tensor(out=osb[:, j * O:(j + 1) * O], in0=yy[:, (first + j) * O:(first + j + 1) * O],
+                                               scalar=rstds[c // 2][:, k:k + 1], in1=b_b[:], op0=ALU.mult, op1=ALU.add)
+            nc.sync.dma_start(out=out_v[:, c * G * O:(c + 1) * G * O], in_=osb[:])
 
         craw4 = craw[:].rearrange("p (t o d) -> p t o d", t=4, o=O, d=6)
         cg = const.tile([P, DEG * 4 * O], BF16, name="cg", align_bytes=64)
@@ -296,97 +367,141 @@ def tile_gottliebkanlayer_t_kernel(tc, x, alpha, coeffs, ln_weight, ln_bias, out
         sigmoid(0)
         sigmoid(1)
         z_transposes(0)
+        sigmoid(2)
+        L = NCH - 1
 
         def live(c):
             return 0 <= c < NCH
 
-        for k in range(NCH):
-            if live(k - 2):
-                mx(k - 2)
-            square_w3(k)
-            t1_scalar(k)
-            if live(k + 1):
-                z_transposes(k + 1)
-            if live(k - 2):
-                evacuate(k - 2)
-            square_p4(k)
-            for j in range(G):
-                if live(k - 5):
-                    final(k - 5, yys[k - 1], G, j)
-            if live(k - 3):
-                stats(k - 3, yys[k - 1])
-            if live(k - 2):
-                yys[k] = psy.tile([P, 2 * G * O], F32, name="yy")
-                y_transposes(k - 2, yys[k])
-                if live(k - 4):
-                    centre(k - 4, yys[k], G)
-            if live(k + 2):
-                sigmoid(k + 2)
-            if live(k + 5):
-                load_x(k + 5)
-            square_p5(k)
-            if live(k - 1):
-                t2_gpsimd(k - 1)
+        def new_yt():
+            return psy.tile([P, NW], F32, name="yt")
+
+        for k in range(L):
             if live(k - 4):
-                rstd_of(k - 4)
+                evacuate(both(k - 4))
+            square_w3(both(k))
+            t1_scalar(k)
+            z_transposes(k + 1)
+            if live(k - 3):
+                mx(both(k - 3), new_yt())
+            square_p4(both(k))
+            square_p5(both(k))
+            if live(k - 9):
+                final(k - 9, yys[k - 1], G)
+            if live(k - 5):
+                stats(k - 5, yys[k - 1])
+            if live(k - 4):
+                yys[k] = psy.tile([P, 2 * G * O], F32, name="yy")
+                y_transposes(k - 4, yys[k])
+                if live(k - 8):
+                    centre(k - 8, yys[k], G)
+            if k >= 1 and live(k + 2):
+                sigmoid(k + 2)
+            if live(k + 6):
+                load_x(k + 6)
+            if k % 2 == 1:
+                g = k // 2
+                new_odd(g)
+                new_even(g, one, "even")
+                t2_gpsimd(g)
+                if live(2 * (g - 3)):
+                    rstd_of(g - 3)
+                t4_gpsimd(g)
             if live(k - 1):
-                t4_gpsimd(k - 1)
-            for r in range(G):
-                if live(k - 1):
-                    t3_t5(k - 1, 3, r)
-            if live(k - 1):
-                t3_t5(k - 1, 5, 0)
-                t3_t5(k - 1, 5, 1)
-                t1_vector(k - 1)
+                vector_odd(both(k - 1))
             if k == 1:
                 coefficient_work()
-            if live(k - 1):
-                quantise(k - 1, t1s[k - 1], 1, 1)
-            if live(k - 3):
-                add_eps(k - 3)
-            if live(k - 1):
-                quantise(k - 1, tbs[k - 1], 2, 5)
+            if k % 2 == 0 and k >= 2:
+                g = k // 2 - 1
+                quantise_t1(range(FIRST[g], FIRST[g] + SIZES[g]))
+                quantise_odd(g)
+                if live(k - 6):
+                    add_eps((k - 6) // 2)
+                quantise_even(g)
 
-        L = NCH - 1
-        mx(L - 1)
-        evacuate(L - 1)
-        for j in range(G):
-            final(L - 4, yys[L], G, j)
-        stats(L - 2, yys[L])
-        late = psy.tile([P, 2 * G * O], F32, name="yy")
-        centre(L - 3, late, 0)
-        centre(L - 2, late, G)
-        own1 = psz.tile([P, I], F32, name="zp")
-        y_transposes(L - 1, own1)
-        centre(L - 1, own1, G)
-        t2_gpsimd(L)
-        rstd_of(L - 3)
-        t4_gpsimd(L)
-        for r in range(G):
-            t3_t5(L, 3, r)
-        for r in range(G):
-            t3_t5(L, 5, r)
-        t1_vector(L)
-        stats(L - 1, own1)
-        quantise(L, t1s[L], 1, 1)
-        add_eps(L - 2)
-        add_eps(L - 1)
-        quantise(L, tbs[L], 2, 5)
-        rstd_of(L - 2)
-        rstd_of(L - 1)
-        mx(L)
-        evacuate(L)
-        own0 = psz.tile([P, I], F32, name="zp")
-        y_transposes(L, own0)
-        centre(L, own0, G)
-        for j in range(G):
-            final(L - 3, late, 0, j)
-        for j in range(G):
-            final(L - 2, late, G, j)
-        for j in range(G):
-            final(L - 1, own1, G, j)
-        stats(L, own0)
-        add_eps(L)
-        rstd_of(L)
-        for j in range(G):
-            final(L, own0, G, j)
+        A, C = range(NT - 2, NT - 1), range(NT - 1, NT)
+        g30, gA, gC = NG - 3, NG - 2, NG - 1
+        evacuate(both(L - 4))
+        square_w3(A)
+        mx(both(L - 3), new_yt())
+        square_p4(A)
+        square_p5(A)
+        final(L - 9, yys[L - 1], G)
+        stats(L - 5, yys[L - 1])
+        own = {}
+
+        def own_bank(c):
+            own[c] = psz.tile([P, I], F32, name="zp")
+            y_transposes(c, own[c])
+            centre(c, own[c], G)
+
+        own_bank(L - 4)
+        bank0 = psy.tile([P, 2 * G * O], F32, name="yy")
+        centre(L - 8, bank0, 0)
+        centre(L - 7, bank0, G)
+        evacuate(both(L - 3))
+        mx(both(L - 2), new_yt())
+        own_bank(L - 3)
+        new_odd(g30)
+        new_even(g30, one, "even")
+        t2_gpsimd(g30)
+        rstd_of(12)
+        t4_gpsimd(g30)
+        vector_odd(both(L - 1))
+        stats(L - 4, own[L - 4])
+        quantise_t1(both(L - 1))
+        quantise_odd(g30)
+        add_eps(13)
+        quantise_even(g30)
+
+        square_w3(C)
+        square_p4(C)
+        square_p5(C)
+        t1_scalar(L)
+        evacuate(both(L - 2))
+        mx(both(L - 1), new_yt())
+        own_bank(L - 2)
+        for g in (gA, gC):
+            new_odd(g)
+            new_even(g, work, "last")
+        t2_gpsimd(gA)
+        rstd_of(13)
+        t4_gpsimd(gA)
+        t2_gpsimd(gC)
+        t4_gpsimd(gC)
+        final(L - 8, bank0, 0)
+        final(L - 7, bank0, G)
+        bank1 = psy.tile([P, 2 * G * O], F32, name="yy")
+        centre(L - 6, bank1, 0)
+        centre(L - 5, bank1, G)
+        vector_odd(A)
+        stats(L - 3, own[L - 3])
+        quantise_odd(gA)
+        quantise_even(gA)
+        evacuate(both(L - 1))
+        own_bank(L - 1)
+        vector_odd(C)
+        stats(L - 2, own[L - 2])
+        quantise_t1(both(L))
+        quantise_odd(gC)
+        add_eps(14)
+        quantise_even(gC)
+        rstd_of(14)
+        mx(A, new_yt())
+        mx(C, psz.tile([P, I], F32, name="zp"))
+        evacuate(A)
+        evacuate(C)
+        stats(L - 1, own[L - 1])
+        final(L - 6, bank1, 0)
+        add_eps(15, 0, 1)
+        final(L - 5, bank1, G)
+        rstd_of(15, 0, 1)
+        own_bank(L)
+        final(L - 4, own[L - 4], G)
+        final(L - 3, own[L - 3], G)
+        stats(L, own[L])
+        final(L - 2, own[L - 2], G)
+        add_eps(15, 1, 2)
+        rstd_of(15, 1, 2)
+        final(L - 1, own[L - 1], G)
+        final(L, own[L], G)

@@ -25,7 +25,7 @@ FIRST = tuple(sum(SIZES[:g]) for g in range(NG))
 GROUP_OF = tuple(g for g in range(NG) for n in range(SIZES[g]))
 T1_FIRST = tuple(min(FIRST[GROUP_OF[q]], NT - 2) for q in range(NT))
 assert sum(SIZES) == NT
-T1_SCALAR_ROWS = (1, 0) * (NCH // 2 - 2) + (1,) + (2,) * 3
+T1_SCALAR_ROWS = (0, 1, 1, 1, 1, 1, 1) * 4 + (1,) + (2,) * 3
 LN_EPS = 1e-5
 FLOPS = 2 * B * I * O * DEG
 
@@ -39,6 +39,7 @@ def tile_gottliebkanlayer_t_kernel(tc, x, alpha, coeffs, ln_weight, ln_bias, out
         xin = ctx.enter_context(tc.tile_pool(name="xin", bufs=6))
         work = ctx.enter_context(tc.tile_pool(name="work", bufs=3))
         ahead = ctx.enter_context(tc.tile_pool(name="ahead", bufs=3))
+        coded = ctx.enter_context(tc.tile_pool(name="coded", bufs=4))
         one = ctx.enter_context(tc.tile_pool(name="one", bufs=1))
         stat = ctx.enter_context(tc.tile_pool(name="stat", bufs=8))
         psz = ctx.enter_context(tc.psum_pool(name="psz", bufs=3 * G))
@@ -73,10 +74,13 @@ def tile_gottliebkanlayer_t_kernel(tc, x, alpha, coeffs, ln_weight, ln_bias, out
         powe = const.tile([P, 2], F32, name="powe")
         for k, lo in enumerate((1e-4, 6e-3, 5e-2)):
             nc.vector.memset(floors[:, k:k + 1], lo)
-        for k, ex in enumerate((0.5, -0.5)):
+        for k, ex in enumerate((0.25, -0.5)):
             nc.vector.memset(powe[:, k:k + 1], ex)
         mhalf = const.tile([P, 2 * G], F32, name="mhalf")
         nc.vector.memset(mhalf[:], -0.5)
+        eps = const.tile([P, 1], F32, name="eps")
+        nc.vector.memset(eps[:], LN_EPS)
+        warm = const.tile([P, 1], F32, name="warm")
         ones = const.tile([P, 64], BF16, name="ones")
         nc.vector.memset(ones[:], 1.0)
         ident = const.tile([P, P], F32, name="ident")
@@ -85,7 +89,7 @@ def tile_gottliebkanlayer_t_kernel(tc, x, alpha, coeffs, ln_weight, ln_bias, out
         names = ("a0", "a2", "a6", "a1", "a2b", "a2c", "a3", "a4", "a8", "p01", "a2sq", "c40", "c42", "c31", "c33",
                  "c44", "c55", "c51", "c53", "h3", "h4", "h5", "sg3", "sg4", "sg5", "aa3", "aa4", "aa5", "ab3", "ab4",
                  "ab5", "r3", "r4", "r5", "v3", "t1", "u0", "u1", "w0", "w1", "m2", "e3", "x1", "b4", "yy", "k4", "mm",
-                 "m4", "t5", "b5", "nt", "e5", "s5", "c11", "c20")
+                 "m4", "t5", "b5", "nt", "e5", "s5", "c11", "c20", "sq3")
         sc = const.tile([P, len(names)], F32, name="sc")
         idx = dict((n, k) for k, n in enumerate(names))
 
@@ -107,18 +111,16 @@ def tile_gottliebkanlayer_t_kernel(tc, x, alpha, coeffs, ln_weight, ln_bias, out
         gp = const.tile([P, 2], F32, name="gp")
         s3 = gp[:, 0:1]
         ir5 = gp[:, 1:2]
-        ts(col("h3"), col("c33"), 0.0, 0.5, ALU.is_ge, ALU.subtract)
-        stt(col("aa3"), col("c33"), 2.0, col("h3"), ALU.mult, ALU.mult)
-        nc.vector.tensor_tensor(out=col("ab3"), in0=col("aa3"), in1=floors[:, 0:1], op=ALU.max)
-        nc.gpsimd.tensor_tensor(out=s3, in0=col("ab3"), in1=powe[:, 0:1], op=ALU.pow)
+        ts(col("sq3"), col("c33"), col("c33"), 1e-8, ALU.mult, ALU.max)
+        nc.gpsimd.tensor_tensor(out=s3, in0=col("sq3"), in1=powe[:, 0:1], op=ALU.pow)
         ts(col("c44"), col("c33"), col("a3"), 2.0)
         ts(col("c11"), col("a0"), 2.0)
         ts(col("c55"), col("c44"), col("a4"), 2.0)
         ts(col("c20"), col("a2"), -1.0)
         c20 = col("c20")
-        ts(col("h4", 2), col("c44", 2), 0.0, 0.5, ALU.is_ge, ALU.subtract)
-        stt(col("aa4", 2), col("c44", 2), 2.0, col("h4", 2), ALU.mult, ALU.mult)
-        nc.vector.tensor_tensor(out=col("ab4", 2), in0=col("aa4", 2), in1=floors[:, 1:3], op=ALU.max)
+        ts(col("h3", 3), col("c33", 3), 0.0, 0.5, ALU.is_ge, ALU.subtract)
+        stt(col("aa3", 3), col("c33", 3), 2.0, col("h3", 3), ALU.mult, ALU.mult)
+        nc.vector.tensor_tensor(out=col("ab3", 3), in0=col("aa3", 3), in1=floors[:], op=ALU.max)
         nc.gpsimd.tensor_tensor(out=ir5, in0=col("ab5"), in1=powe[:, 1:2], op=ALU.pow)
         ts(col("sg3", 3), col("h3", 3), 2.0)
         nc.vector.reciprocal(out=col("r3", 3), in_=col("ab3", 3))
@@ -182,15 +184,17 @@ def tile_gottliebkanlayer_t_kernel(tc, x, alpha, coeffs, ln_weight, ln_bias, out
 
         def sigmoid(c):
             zn = ahead.tile([P, CW], F32, name="zn")
-            nc.scalar.activation(out=zn[:].rearrange("p (r t q) -> p r t q", r=G, t=4),
-                                 in_=x_tiles[c][:].rearrange("p (r q t) -> p r t q", r=G, t=4), func=ACT.Sigmoid)
+            m = 1 if c == 0 else G
+            for r in range(0, G, m):
+                cols = slice(r * I, (r + m) * I)
+                nc.scalar.activation(out=zn[:, cols], in_=x_tiles[c][:, cols], func=ACT.Sigmoid)
             zns[c] = zn
 
         def z_transposes(c):
             for r in range(G):
                 zp = psz.tile([P, I], F32, name="zp")
                 for t in range(4):
-                    nc.tensor.transpose(zp[:, t * P:(t + 1) * P], zns[c][:, (r * 4 + t) * P:(r * 4 + t + 1) * P], ident[:])
+                    nc.tensor.transpose(zp[:, t * P:(t + 1) * P], zns[c][:, r * I + t:(r + 1) * I:4], ident[:])
                 zps[G * c + r] = zp
 
         def square_w3(qs):
@@ -226,7 +230,7 @@ def tile_gottliebkanlayer_t_kernel(tc, x, alpha, coeffs, ln_weight, ln_bias, out
             odds[g] = work.tile([P, 2 * GMAX * I], BF16, name="odd", align_bytes=64)
 
         def new_even(g, pool, name):
-            evens[g] = pool.tile([P, 2 * GMAX * I], BF16, name=name, align_bytes=64)
+            evens[g] = pool.tile([P, 2 * SIZES[g] * I], BF16, name=name, align_bytes=64)
 
         def t3_t5(q, d):
             g = GROUP_OF[q]
@@ -248,36 +252,38 @@ def tile_gottliebkanlayer_t_kernel(tc, x, alpha, coeffs, ln_weight, ln_bias, out
                                     op0=ALU.mult, op1=ALU.add)
 
         def vector_odd(qs):
-            for q in reversed(qs):
-                t3_t5(q, 5)
-            if len(qs) == G:
-                t1_vector(qs.start // G)
-            for q in reversed(qs):
-                t3_t5(q, 3)
+            degrees = (5, 1, 3) if qs.start > 0 else (1, 3, 5)
+            for d in degrees:
+                if d == 1 and len(qs) == G:
+                    t1_vector(qs.start // G)
+                for q in reversed(qs):
+                    if d > 1:
+                        t3_t5(q, d)
 
-        def quantised(src, width):
-            cod = work.tile([P, width // 4], U32, name="cod%d" % width, align_bytes=64)
-            scl = work.tile([P, width // 4], U8, name="scl%d" % width, align_bytes=64)
+        def quantised(src, width, kind):
+            words = width // 4
+            cod = coded.tile([P, words], U32, name="cod_" + kind, align_bytes=64)
+            scl = coded.tile([P, words], U8, name="scl_" + kind, align_bytes=64)
             nc.vector.quantize_mx(out=cod[:].bitcast(FP8X4), scales=scl[:], in_=src[:, 0:width])
             return cod, scl
 
         def quantise_t1(qs):
-            cod, scl = quantised(t1s[qs.start], len(qs) * I)
+            cod, scl = quantised(t1s[qs.start], len(qs) * I, "t1")
             for q in qs:
                 codes[(q, 1)] = (cod, scl, (q - qs.start) * P)
 
-        def quantise_pair(g, tiles, degrees):
+        def quantise_pair(g, tiles, degrees, kind):
             size = SIZES[g]
-            cod, scl = quantised(tiles[g], 2 * size * I)
+            cod, scl = quantised(tiles[g], 2 * size * I, kind)
             for h, d in enumerate(degrees):
                 for q in range(FIRST[g], FIRST[g] + size):
                     codes[(q, d)] = (cod, scl, (h * size + q - FIRST[g]) * P)
 
         def quantise_odd(g):
-            quantise_pair(g, odds, (3, 5))
+            quantise_pair(g, odds, (3, 5), "odd")
 
         def quantise_even(g):
-            quantise_pair(g, evens, (2, 4))
+            quantise_pair(g, evens, (2, 4), "even")
 
         def mx(qs, yt):
             for n, d in enumerate((1, 3, 5, 2, 4)):
@@ -367,7 +373,6 @@ def tile_gottliebkanlayer_t_kernel(tc, x, alpha, coeffs, ln_weight, ln_bias, out
         sigmoid(0)
         sigmoid(1)
         z_transposes(0)
-        sigmoid(2)
         L = NCH - 1
 
         def live(c):
@@ -395,7 +400,7 @@ def tile_gottliebkanlayer_t_kernel(tc, x, alpha, coeffs, ln_weight, ln_bias, out
                 y_transposes(k - 4, yys[k])
                 if live(k - 8):
                     centre(k - 8, yys[k], G)
-            if k >= 1 and live(k + 2):
+            if live(k + 2):
                 sigmoid(k + 2)
             if live(k + 6):
                 load_x(k + 6)
@@ -479,13 +484,14 @@ def tile_gottliebkanlayer_t_kernel(tc, x, alpha, coeffs, ln_weight, ln_bias, out
         quantise_odd(gA)
         quantise_even(gA)
         evacuate(both(L - 1))
+        nc.scalar.activation(out=warm[:], in_=eps[:], func=ACT.Abs_reciprocal_sqrt)
         own_bank(L - 1)
         vector_odd(C)
-        stats(L - 2, own[L - 2])
         quantise_t1(both(L))
         quantise_odd(gC)
-        add_eps(14)
         quantise_even(gC)
+        stats(L - 2, own[L - 2])
+        add_eps(14)
         rstd_of(14)
         mx(A, new_yt())
         mx(C, psz.tile([P, I], F32, name="zp"))
@@ -501,7 +507,7 @@ def tile_gottliebkanlayer_t_kernel(tc, x, alpha, coeffs, ln_weight, ln_bias, out
         final(L - 3, own[L - 3], G)
         stats(L, own[L])
         final(L - 2, own[L - 2], G)
-        add_eps(15, 1, 2)
-        rstd_of(15, 1, 2)
+        nc.scalar.activation(out=rstds[15][:, G:2 * G], in_=sts[15][:, G:2 * G, 2], func=ACT.Abs_reciprocal_sqrt,
+                             scale=1.0 / O, bias=eps[:])
         final(L - 1, own[L - 1], G)
         final(L, own[L], G)

@@ -25,7 +25,7 @@ FIRST = tuple(sum(SIZES[:g]) for g in range(NG))
 GROUP_OF = tuple(g for g in range(NG) for n in range(SIZES[g]))
 T1_FIRST = tuple(min(FIRST[GROUP_OF[q]], NT - 2) for q in range(NT))
 assert sum(SIZES) == NT
-T1_SCALAR_ROWS = (0, 1, 1, 1, 1, 1, 1) * 4 + (1,) + (2,) * 3
+T1_SCALAR_ROWS = (0, 1, 1, 1) * 7 + (1,) + (2,) * 3
 LN_EPS = 1e-5
 FLOPS = 2 * B * I * O * DEG
 
@@ -63,8 +63,8 @@ def tile_gottliebkanlayer_t_kernel(tc, x, alpha, coeffs, ln_weight, ln_bias, out
             load_x(c)
         g_b = const.tile([P, O], BF16, name="g_b")
         nc.sync.dma_start(out=g_b[:], in_=ln_weight.partition_broadcast(P))
-        b_b = const.tile([P, O], BF16, name="b_b")
-        nc.sync.dma_start(out=b_b[:], in_=ln_bias.partition_broadcast(P))
+        b_b = const.tile([P, G * O], BF16, name="b_b")
+        nc.sync.dma_start(out=b_b[:, 0:O], in_=ln_bias.partition_broadcast(P))
 
         cst0 = const.tile([P, 9], F32, name="cst0")
         nc.vector.memset(cst0[:], 2.0)
@@ -329,12 +329,30 @@ def tile_gottliebkanlayer_t_kernel(tc, x, alpha, coeffs, ln_weight, ln_bias, out
             cols = slice(h0 * G, h1 * G)
             nc.gpsimd.tensor_tensor(out=rstds[m][:, cols], in0=ves[m][:, cols], in1=mhalf[:, cols], op=ALU.pow)
 
+        def rstd_by_scalar(c):
+            cols = slice((c % 2) * G, (c % 2 + 1) * G)
+            nc.scalar.activation(out=rstds[c // 2][:, cols], in_=sts[c // 2][:, cols, 2], func=ACT.Abs_reciprocal_sqrt,
+                                 scale=1.0 / O, bias=eps[:])
+
         def final(c, yy, first):
             osb = stat.tile([P, G * O], F32, name="osb")
             for j in range(G):
                 k = (c % 2) * G + j
                 nc.vector.scalar_tensor_tensor(out=osb[:, j * O:(j + 1) * O], in0=yy[:, (first + j) * O:(first + j + 1) * O],
-                                               scalar=rstds[c // 2][:, k:k + 1], in1=b_b[:], op0=ALU.mult, op1=ALU.add)
+                                               scalar=rstds[c // 2][:, k:k + 1], in1=b_b[:, 0:O], op0=ALU.mult, op1=ALU.add)
+            nc.sync.dma_start(out=out_v[:, c * G * O:(c + 1) * G * O], in_=osb[:])
+
+        def scaled_by_scalar(c, yy, first):
+            tmp = stat.tile([P, G * O], F32, name="tmp")
+            for j in range(G):
+                k = (c % 2) * G + j
+                nc.scalar.activation(out=tmp[:, j * O:(j + 1) * O], in_=yy[:, (first + j) * O:(first + j + 1) * O],
+                                     func=ACT.Copy, scale=rstds[c // 2][:, k:k + 1])
+            return tmp
+
+        def biased_by_gpsimd(c, tmp):
+            osb = stat.tile([P, G * O], F32, name="osb")
+            nc.gpsimd.tensor_tensor(out=osb[:], in0=tmp[:], in1=b_b[:], op=ALU.add)
             nc.sync.dma_start(out=out_v[:, c * G * O:(c + 1) * G * O], in_=osb[:])
 
         craw4 = craw[:].rearrange("p (t o d) -> p t o d", t=4, o=O, d=6)
@@ -367,6 +385,7 @@ def tile_gottliebkanlayer_t_kernel(tc, x, alpha, coeffs, ln_weight, ln_bias, out
                 nc.tensor.matmul(out=ps0[:], lhsT=craw4[:, t, :, 0], rhs=ones[:], start=(t == 0),
                                  stop=(t == 3))
             nc.vector.tensor_copy(out=y0[:], in_=ps0[:, 0:1])
+            nc.vector.tensor_copy(out=b_b[:, O:2 * O], in_=b_b[:, 0:O])
             ts(cen[:], ident[:], -1.0 / O, op0=ALU.add)
             nc.vector.tensor_tensor(out=ceng[:], in0=cen[:], in1=g_b[:], op=ALU.mult)
 
@@ -486,6 +505,8 @@ def tile_gottliebkanlayer_t_kernel(tc, x, alpha, coeffs, ln_weight, ln_bias, out
         evacuate(both(L - 1))
         nc.scalar.activation(out=warm[:], in_=eps[:], func=ACT.Abs_reciprocal_sqrt)
         own_bank(L - 1)
+        parts = [scaled_by_scalar(L - 6, bank1, 0), scaled_by_scalar(L - 5, bank1, G)]
+        biased_by_gpsimd(L - 6, parts[0])
         vector_odd(C)
         quantise_t1(both(L))
         quantise_odd(gC)
@@ -493,21 +514,18 @@ def tile_gottliebkanlayer_t_kernel(tc, x, alpha, coeffs, ln_weight, ln_bias, out
         stats(L - 2, own[L - 2])
         add_eps(14)
         rstd_of(14)
+        biased_by_gpsimd(L - 5, parts[1])
         mx(A, new_yt())
         mx(C, psz.tile([P, I], F32, name="zp"))
         evacuate(A)
         evacuate(C)
         stats(L - 1, own[L - 1])
-        final(L - 6, bank1, 0)
-        add_eps(15, 0, 1)
-        final(L - 5, bank1, G)
-        rstd_of(15, 0, 1)
-        own_bank(L)
+        rstd_by_scalar(L - 1)
         final(L - 4, own[L - 4], G)
+        own_bank(L)
         final(L - 3, own[L - 3], G)
         stats(L, own[L])
         final(L - 2, own[L - 2], G)
-        nc.scalar.activation(out=rstds[15][:, G:2 * G], in_=sts[15][:, G:2 * G, 2], func=ACT.Abs_reciprocal_sqrt,
-                             scale=1.0 / O, bias=eps[:])
+        rstd_by_scalar(L)
         final(L - 1, own[L - 1], G)
         final(L, own[L], G)

from contextlib import ExitStack

import concourse.mybir as mybir
from concourse.masks import make_identity

F32 = mybir.dt.float32
BF16 = mybir.dt.bfloat16
U32 = mybir.dt.uint32
U8 = mybir.dt.uint8
FP8X4 = mybir.dt.float8_e4m3fn_x4
ALU = mybir.AluOpType
ACT = mybir.ActivationFunctionType

P = 128
B, I, O, DEG = 8192, 512, 128, 5
NT = B // P
G = 2
NCH = NT // G
CW = G * I
NW = G * P
GMAX = 4
SIZES = (GMAX,) * 15 + (2, 1, 1)
NG = len(SIZES)
FIRST = tuple(sum(SIZES[:g]) for g in range(NG))
GROUP_OF = tuple(g for g in range(NG) for n in range(SIZES[g]))
T1_FIRST = tuple(min(FIRST[GROUP_OF[q]], NT - 2) for q in range(NT))
assert sum(SIZES) == NT
T1_SCALAR_ROWS = (0, 1, 1, 1) * 7 + (1,) + (2,) * 3
LN_EPS = 1e-5
FLOPS = 2 * B * I * O * DEG


def tile_gottliebkanlayer_t_kernel(tc, x, alpha, coeffs, ln_weight, ln_bias, out):
    nc = tc.nc
    x_v = x.rearrange("(p t) i -> p (t i)", t=NT)
    out_v = out.rearrange("(p t) o -> p (t o)", t=NT)
    with ExitStack() as ctx:
        const = ctx.enter_context(tc.tile_pool(name="const", bufs=1))
        xin = ctx.enter_context(tc.tile_pool(name="xin", bufs=6))
        work = ctx.enter_context(tc.tile_pool(name="work", bufs=3))
        ahead = ctx.enter_context(tc.tile_pool(name="ahead", bufs=3))
        coded = ctx.enter_context(tc.tile_pool(name="coded", bufs=4))
        one = ctx.enter_context(tc.tile_pool(name="one", bufs=1))
        stat = ctx.enter_context(tc.tile_pool(name="stat", bufs=8))
        psz = ctx.enter_context(tc.psum_pool(name="psz", bufs=3 * G))
        psy = ctx.enter_context(tc.psum_pool(name="psy", bufs=1))
        ctx.enter_context(tc.manual_schedule())

        x_tiles = {}

        def load_x(c):
            x_sb = xin.tile([P, CW], BF16, name="x_sb")
            nc.sync.dma_start(out=x_sb[:], in_=x_v[:, c * CW:(c + 1) * CW])
            x_tiles[c] = x_sb

        a_bf = const.tile([P, 1], BF16, name="a_bf")
        nc.sync.dma_start(out=a_bf[:], in_=alpha.partition_broadcast(P))
        load_x(0)
        load_x(1)
        craw = const.tile([P, 4 * O * 6], BF16, name="craw")
        nc.sync.dma_start(out=craw[:], in_=coeffs.rearrange("(q t) o d -> q (t o d)", t=4))
        for c in range(2, 6):
            load_x(c)
        g_b = const.tile([P, O], BF16, name="g_b")
        nc.sync.dma_start(out=g_b[:], in_=ln_weight.partition_broadcast(P))
        b_b = const.tile([P, G * O], BF16, name="b_b")
        nc.sync.dma_start(out=b_b[:, 0:O], in_=ln_bias.partition_broadcast(P))

        cst0 = const.tile([P, 9], F32, name="cst0")
        nc.vector.memset(cst0[:], 2.0)
        for k, v in ((0, 0.0), (2, 6.0), (3, 1.0), (6, 3.0), (7, 4.0), (8, 8.0)):
            nc.vector.memset(cst0[:, k:k + 1], v)
        floors = const.tile([P, 3], F32, name="floors")
        powe = const.tile([P, 2], F32, name="powe")
        for k, lo in enumerate((1e-4, 6e-3, 5e-2)):
            nc.vector.memset(floors[:, k:k + 1], lo)
        for k, ex in enumerate((0.25, -0.5)):
            nc.vector.memset(powe[:, k:k + 1], ex)
        mhalf = const.tile([P, 2 * G], F32, name="mhalf")
        nc.vector.memset(mhalf[:], -0.5)
        eps = const.tile([P, 1], F32, name="eps")
        nc.vector.memset(eps[:], LN_EPS)
        warm = const.tile([P, 1], F32, name="warm")
        ones = const.tile([P, 64], BF16, name="ones")
        nc.vector.memset(ones[:], 1.0)
        ident = const.tile([P, P], F32, name="ident")
        make_identity(nc, ident[:])

        names = ("a0", "a2", "a6", "a1", "a2b", "a2c", "a3", "a4", "a8", "p01", "a2sq", "c40", "c42", "c31", "c33",
                 "c44", "c55", "c51", "c53", "h3", "h4", "h5", "sg3", "sg4", "sg5", "aa3", "aa4", "aa5", "ab3", "ab4",
                 "ab5", "r3", "r4", "r5", "v3", "t1", "u0", "u1", "w0", "w1", "m2", "e3", "x1", "b4", "yy", "k4", "mm",
                 "m4", "t5", "b5", "nt", "e5", "s5", "c11", "c20", "sq3")
        sc = const.tile([P, len(names)], F32, name="sc")
        idx = dict((n, k) for k, n in enumerate(names))

        def col(n, w=1):
            return sc[:, idx[n]:idx[n] + w]

        def ts(o, i, s1, s2=None, op0=ALU.mult, op1=ALU.mult):
            if s2 is None:
                nc.vector.tensor_scalar(out=o, in0=i, scalar1=s1, scalar2=None, op0=op0)
            else:
                nc.vector.tensor_scalar(out=o, in0=i, scalar1=s1, scalar2=s2, op0=op0, op1=op1)

        def stt(o, i0, s, i1, op0, op1):
            nc.vector.scalar_tensor_tensor(out=o, in0=i0, scalar=s, in1=i1, op0=op0, op1=op1)

        ts(col("a0", 9), cst0[:], a_bf[:, 0:1], op0=ALU.add)
        nc.vector.tensor_tensor(out=col("p01", 3), in0=col("a0", 3), in1=col("a1", 3), op=ALU.mult)
        stt(col("c33"), col("p01"), 8.0, col("a2"), ALU.mult, ALU.mult)
        gp = const.tile([P, 2], F32, name="gp")
        s3 = gp[:, 0:1]
        ir5 = gp[:, 1:2]
        ts(col("sq3"), col("c33"), col("c33"), 1e-8, ALU.mult, ALU.max)
        nc.gpsimd.tensor_tensor(out=s3, in0=col("sq3"), in1=powe[:, 0:1], op=ALU.pow)
        ts(col("c44"), col("c33"), col("a3"), 2.0)
        ts(col("c11"), col("a0"), 2.0)
        ts(col("c55"), col("c44"), col("a4"), 2.0)
        ts(col("c20"), col("a2"), -1.0)
        c20 = col("c20")
        ts(col("h3", 3), col("c33", 3), 0.0, 0.5, ALU.is_ge, ALU.subtract)
        stt(col("aa3", 3), col("c33", 3), 2.0, col("h3", 3), ALU.mult, ALU.mult)
        nc.vector.tensor_tensor(out=col("ab3", 3), in0=col("aa3", 3), in1=floors[:], op=ALU.max)
        nc.gpsimd.tensor_tensor(out=ir5, in0=col("ab5"), in1=powe[:, 1:2], op=ALU.pow)
        ts(col("sg3", 3), col("h3", 3), 2.0)
        nc.vector.reciprocal(out=col("r3", 3), in_=col("ab3", 3))
        ts(col("c31"), col("a2sq"), -4.0, 8.0, ALU.mult, ALU.add)
        ts(col("v3"), col("p01"), col("a6"), -4.0)
        ts(col("t1"), col("c31"), col("a3"), 2.0)
        nc.vector.tensor_tensor(out=col("c42"), in0=col("t1"), in1=col("v3"), op=ALU.add)
        ts(col("m2"), col("p01"), col("r3"), 4.0)
        ts(col("e3"), col("c31"), col("sg3"))
        ts(col("x1"), col("c42"), col("r4"), 0.5)
        ts(col("b4"), col("x1"), col("ab3"), col("sg4"))
        ts(col("u0", 2), col("c40", 2), col("a4"), 2.0)
        ts(col("w0", 2), col("c31", 2), col("a8"))
        nc.vector.tensor_tensor(out=col("c51", 2), in0=col("u0", 2), in1=col("w0", 2), op=ALU.subtract)
        ts(col("t5"), col("c53"), ir5, 0.5)
        ts(col("s5"), col("ab5"), ir5, col("r3"))
        ts(col("b5"), col("t5"), col("sg5"))
        ts(col("yy"), col("x1"), col("c42"), col("sg4"))
        stt(col("k4"), col("yy"), -0.5, col("c40"), ALU.mult, ALU.add)
        ts(col("mm"), col("r3"), col("r3"), col("ab4"))
        ts(col("m4"), col("mm"), col("sg4"))
        ts(col("nt"), col("t5"), col("t5"), -1.0)
        stt(col("e5"), col("c51"), col("sg5"), col("nt"), ALU.mult, ALU.add)

        zns = {}
        zps = {}
        w3s = {}
        p4s = {}
        p5s = {}
        odds = {}
        evens = {}
        t1s = {}
        codes = {}
        yts = {}
        ysbs = {}
        yys = {}
        sts = {}
        ves = {}
        rstds = {}

        def both(c):
            return range(G * c, G * (c + 1))

        def columns(qs):
            first = FIRST[GROUP_OF[qs.start]]
            return slice((qs.start - first) * I, (qs.stop - first) * I)

        def by_row(ap):
            return ap.rearrange("p (t n) -> p n t", t=4)

        def rows_of(ap):
            return ap.rearrange("p (n t) -> p n t", t=4)

        def one_row(q):
            return columns(range(q, q + 1))

        def group_tile(tiles, g, name):
            if g not in tiles:
                tiles[g] = work.tile([P, GMAX * I], F32, name=name)
            return tiles[g]

        def sigmoid(c):
            zn = ahead.tile([P, CW], F32, name="zn")
            m = 1 if c == 0 else G
            for r in range(0, G, m):
                cols = slice(r * I, (r + m) * I)
                nc.scalar.activation(out=zn[:, cols], in_=x_tiles[c][:, cols], func=ACT.Sigmoid)
            zns[c] = zn

        def z_transposes(c):
            for r in range(G):
                zp = psz.tile([P, I], F32, name="zp")
                for t in range(4):
                    nc.tensor.transpose(zp[:, t * P:(t + 1) * P], zns[c][:, r * I + t:(r + 1) * I:4], ident[:])
                zps[G * c + r] = zp

        def square_w3(qs):
            w3 = group_tile(w3s, GROUP_OF[qs.start], "w3")
            for q in reversed(qs):
                nc.scalar.activation(out=rows_of(w3[:, one_row(q)]), in_=by_row(zps[q][:]), func=ACT.Square, scale=s3)

        def square_p4(qs):
            g, cols = GROUP_OF[qs.start], columns(qs)
            nc.scalar.activation(out=group_tile(p4s, g, "p4")[:, cols], in_=w3s[g][:, cols], func=ACT.Square,
                                 bias=col("b4"))

        def square_p5(qs):
            g, cols = GROUP_OF[qs.start], columns(qs)
            nc.scalar.activation(out=group_tile(p5s, g, "p5")[:, cols], in_=w3s[g][:, cols], func=ACT.Square,
                                 scale=col("s5"), bias=col("b5"))

        def t1_out(q):
            first = T1_FIRST[q]
            if first not in t1s:
                t1s[first] = work.tile([P, GMAX * I], BF16, name="t1", align_bytes=64)
            return rows_of(t1s[first][:, (q - first) * I:(q - first + 1) * I])

        def t1_scalar(c):
            for q in both(c)[:T1_SCALAR_ROWS[c]]:
                nc.scalar.activation(out=t1_out(q), in_=by_row(zps[q][:]), func=ACT.Copy, scale=col("c11"))

        def t1_vector(c):
            for q in both(c)[T1_SCALAR_ROWS[c]:]:
                ts(t1_out(q), by_row(zps[q][:]), col("c11"))

        def new_odd(g):
            odds[g] = work.tile([P, 2 * GMAX * I], BF16, name="odd", align_bytes=64)

        def new_even(g, pool, name):
            evens[g] = pool.tile([P, 2 * SIZES[g] * I], BF16, name=name, align_bytes=64)

        def t3_t5(q, d):
            g = GROUP_OF[q]
            src, add = {3: (w3s[g], col("e3")), 5: (p5s[g], col("e5"))}[d]
            cols = one_row(q)
            shift = SIZES[g] * I if d == 5 else 0
            nc.vector.scalar_tensor_tensor(out=rows_of(odds[g][:, shift + cols.start:shift + cols.stop]),
                                           in0=rows_of(src[:, cols]), scalar=add, in1=by_row(zps[q][:]),
                                           op0=ALU.add, op1=ALU.mult)

        def t2_gpsimd(g):
            w = SIZES[g] * I
            nc.gpsimd.tensor_scalar(out=evens[g][:, 0:w], in0=w3s[g][:, 0:w], scalar1=col("m2"), scalar2=c20,
                                    op0=ALU.mult, op1=ALU.add)

        def t4_gpsimd(g):
            w = SIZES[g] * I
            nc.gpsimd.tensor_scalar(out=evens[g][:, w:2 * w], in0=p4s[g][:, 0:w], scalar1=col("m4"), scalar2=col("k4"),
                                    op0=ALU.mult, op1=ALU.add)

        def vector_odd(qs):
            degrees = (5, 1, 3) if qs.start > 0 else (1, 3, 5)
            for d in degrees:
                if d == 1 and len(qs) == G:
                    t1_vector(qs.start // G)
                for q in reversed(qs):
                    if d > 1:
                        t3_t5(q, d)

        def quantised(src, width, kind):
            words = width // 4
            cod = coded.tile([P, words], U32, name="cod_" + kind, align_bytes=64)
            scl = coded.tile([P, words], U8, name="scl_" + kind, align_bytes=64)
            nc.vector.quantize_mx(out=cod[:].bitcast(FP8X4), scales=scl[:], in_=src[:, 0:width])
            return cod, scl

        def quantise_t1(qs):
            cod, scl = quantised(t1s[qs.start], len(qs) * I, "t1")
            for q in qs:
                codes[(q, 1)] = (cod, scl, (q - qs.start) * P)

        def quantise_pair(g, tiles, degrees, kind):
            size = SIZES[g]
            cod, scl = quantised(tiles[g], 2 * size * I, kind)
            for h, d in enumerate(degrees):
                for q in range(FIRST[g], FIRST[g] + size):
                    codes[(q, d)] = (cod, scl, (h * size + q - FIRST[g]) * P)

        def quantise_odd(g):
            quantise_pair(g, odds, (3, 5), "odd")

        def quantise_even(g):
            quantise_pair(g, evens, (2, 4), "even")

        def mx(qs, yt):
            for n, d in enumerate((1, 3, 5, 2, 4)):
                cod, scl, first = codes[(qs.start, d)]
                cols = slice(first, first + len(qs) * P)
                nc.tensor.matmul_mx(
                    out=yt[:, 0:len(qs) * P],
                    lhsT=ccod[:, (d - 1) * O:d * O].bitcast(FP8X4), lhsT_scale=cscl[:, (d - 1) * O:d * O],
                    rhs=cod[:, cols].bitcast(FP8X4), rhs_scale=scl[:, cols],
                    start=(n == 0), stop=(n == DEG - 1))
            yts[qs.start] = yt

        def evacuate(qs):
            c = qs.start // G
            if c not in ysbs:
                ysbs[c] = stat.tile([P, NW], F32, name="ysb")
            j = qs.start - G * c
            nc.scalar.activation(out=ysbs[c][:, j * P:(j + len(qs)) * P], in_=yts[qs.start][:, 0:len(qs) * P],
                                 func=ACT.Identity, bias=y0[:, 0:1])

        def y_transposes(c, yy):
            for j in range(G):
                nc.tensor.transpose(yy[:, j * O:(j + 1) * O], ysbs[c][:, j * P:(j + 1) * P], ident[:])

        def centre(c, yy, first):
            for j in range(G):
                nc.tensor.matmul(out=yy[:, (first + j) * O:(first + j + 1) * O], lhsT=ysbs[c][:, j * P:(j + 1) * P],
                                 rhs=ceng[:], start=True, stop=True)

        def stats(c, yy):
            m, h = divmod(c, 2)
            if h == 0:
                sts[m] = stat.tile([P, 2 * G, 3], F32, name="st")
                ves[m] = stat.tile([P, 2 * G], F32, name="ve")
                rstds[m] = stat.tile([P, 2 * G], F32, name="rstd")
            nc.vector.bn_stats(out=sts[m][:, h * G:(h + 1) * G, :].rearrange("p j s -> p (j s)"),
                               in_=yy[:, 0:G * O].rearrange("p (j o) -> p o j", j=G))

        def add_eps(m, h0=0, h1=2):
            ts(ves[m][:, h0 * G:h1 * G], sts[m][:, h0 * G:h1 * G, 2], 1.0 / O, LN_EPS, ALU.mult, ALU.add)

        def rstd_of(m, h0=0, h1=2):
            cols = slice(h0 * G, h1 * G)
            nc.gpsimd.tensor_tensor(out=rstds[m][:, cols], in0=ves[m][:, cols], in1=mhalf[:, cols], op=ALU.pow)

        def rstd_by_scalar(c):
            cols = slice((c % 2) * G, (c % 2 + 1) * G)
            nc.scalar.activation(out=rstds[c // 2][:, cols], in_=sts[c // 2][:, cols, 2], func=ACT.Abs_reciprocal_sqrt,
                                 scale=1.0 / O, bias=eps[:])

        def final(c, yy, first):
            osb = stat.tile([P, G * O], F32, name="osb")
            for j in range(G):
                k = (c % 2) * G + j
                nc.vector.scalar_tensor_tensor(out=osb[:, j * O:(j + 1) * O], in0=yy[:, (first + j) * O:(first + j + 1) * O],
                                               scalar=rstds[c // 2][:, k:k + 1], in1=b_b[:, 0:O], op0=ALU.mult, op1=ALU.add)
            nc.sync.dma_start(out=out_v[:, c * G * O:(c + 1) * G * O], in_=osb[:])

        def scaled_by_scalar(c, yy, first):
            tmp = stat.tile([P, G * O], F32, name="tmp")
            for j in range(G):
                k = (c % 2) * G + j
                nc.scalar.activation(out=tmp[:, j * O:(j + 1) * O], in_=yy[:, (first + j) * O:(first + j + 1) * O],
                                     func=ACT.Copy, scale=rstds[c // 2][:, k:k + 1])
            return tmp

        def biased_by_gpsimd(c, tmp):
            osb = stat.tile([P, G * O], F32, name="osb")
            nc.gpsimd.tensor_tensor(out=osb[:], in0=tmp[:], in1=b_b[:], op=ALU.add)
            nc.sync.dma_start(out=out_v[:, c * G * O:(c + 1) * G * O], in_=osb[:])

        craw4 = craw[:].rearrange("p (t o d) -> p t o d", t=4, o=O, d=6)
        cg = const.tile([P, DEG * 4 * O], BF16, name="cg", align_bytes=64)

        def regroup(eng, d):
            sign = {3: col("sg3"), 5: col("sg5")}.get(d, 1.0)
            eng.tensor_scalar(
                out=cg[:, (d - 1) * 4 * O:d * 4 * O].rearrange("p (o t) -> p o t", t=4),
                in0=craw4[:, :, :, d].rearrange("p t o -> p o t"),
                scalar1=sign, scalar2=1.0, op0=ALU.mult, op1=ALU.mult)

        regroup(nc.gpsimd, 4)
        regroup(nc.gpsimd, 3)
        regroup(nc.gpsimd, 5)
        regroup(nc.vector, 1)
        regroup(nc.vector, 2)
        ccod = const.tile([P, DEG * O], U32, name="ccod", align_bytes=64)
        cscl = const.tile([P, DEG * O], U8, name="cscl", align_bytes=64)
        y0 = const.tile([P, 1], F32, name="y0")
        cen = const.tile([P, O], F32, name="cen")
        ceng = const.tile([P, O], F32, name="ceng")

        def coefficient_work():
            nc.vector.quantize_mx(out=ccod[:, 0:4 * O].bitcast(FP8X4), scales=cscl[:, 0:4 * O], in_=cg[:, 0:16 * O])
            nc.vector.quantize_mx(out=ccod[:, 4 * O:5 * O].bitcast(FP8X4), scales=cscl[:, 4 * O:5 * O],
                                  in_=cg[:, 16 * O:20 * O])
            ps0 = psy.tile([P, 64], F32, name="ps0", tag="yt")
            for t in range(4):
                nc.tensor.matmul(out=ps0[:], lhsT=craw4[:, t, :, 0], rhs=ones[:], start=(t == 0),
                                 stop=(t == 3))
            nc.vector.tensor_copy(out=y0[:], in_=ps0[:, 0:1])
            nc.vector.tensor_copy(out=b_b[:, O:2 * O], in_=b_b[:, 0:O])
            ts(cen[:], ident[:], -1.0 / O, op0=ALU.add)
            nc.vector.tensor_tensor(out=ceng[:], in0=cen[:], in1=g_b[:], op=ALU.mult)

        sigmoid(0)
        sigmoid(1)
        z_transposes(0)
        L = NCH - 1

        def live(c):
            return 0 <= c < NCH

        def new_yt():
            return psy.tile([P, NW], F32, name="yt")

        for k in range(L):
            if live(k - 4):
                evacuate(both(k - 4))
            square_w3(both(k))
            t1_scalar(k)
            z_transposes(k + 1)
            if live(k - 3):
                mx(both(k - 3), new_yt())
            square_p4(both(k))
            square_p5(both(k))
            if live(k - 9):
                final(k - 9, yys[k - 1], G)
            if live(k - 5):
                stats(k - 5, yys[k - 1])
            if live(k - 4):
                yys[k] = psy.tile([P, 2 * G * O], F32, name="yy")
                y_transposes(k - 4, yys[k])
                if live(k - 8):
                    centre(k - 8, yys[k], G)
            if live(k + 2):
                sigmoid(k + 2)
            if live(k + 6):
                load_x(k + 6)
            if k % 2 == 1:
                g = k // 2
                new_odd(g)
                new_even(g, one, "even")
                t2_gpsimd(g)
                if live(2 * (g - 3)):
                    rstd_of(g - 3)
                t4_gpsimd(g)
            if live(k - 1):
                vector_odd(both(k - 1))
            if k == 1:
                coefficient_work()
            if k % 2 == 0 and k >= 2:
                g = k // 2 - 1
                quantise_t1(range(FIRST[g], FIRST[g] + SIZES[g]))
                quantise_odd(g)
                if live(k - 6):
                    add_eps((k - 6) // 2)
                quantise_even(g)

        A, C = range(NT - 2, NT - 1), range(NT - 1, NT)
        g30, gA, gC = NG - 3, NG - 2, NG - 1
        evacuate(both(L - 4))
        square_w3(A)
        mx(both(L - 3), new_yt())
        square_p4(A)
        square_p5(A)
        final(L - 9, yys[L - 1], G)
        stats(L - 5, yys[L - 1])
        own = {}

        def own_bank(c):
            own[c] = psz.tile([P, I], F32, name="zp")
            y_transposes(c, own[c])
            centre(c, own[c], G)

        own_bank(L - 4)
        bank0 = psy.tile([P, 2 * G * O], F32, name="yy")
        centre(L - 8, bank0, 0)
        centre(L - 7, bank0, G)
        evacuate(both(L - 3))
        mx(both(L - 2), new_yt())
        own_bank(L - 3)
        new_odd(g30)
        new_even(g30, one, "even")
        t2_gpsimd(g30)
        rstd_of(12)
        t4_gpsimd(g30)
        vector_odd(both(L - 1))
        stats(L - 4, own[L - 4])
        quantise_t1(both(L - 1))
        quantise_odd(g30)
        add_eps(13)
        quantise_even(g30)

        square_w3(C)
        square_p4(C)
        square_p5(C)
        t1_scalar(L)
        evacuate(both(L - 2))
        mx(both(L - 1), new_yt())
        own_bank(L - 2)
        for g in (gA, gC):
            new_odd(g)
            new_even(g, work, "last")
        t2_gpsimd(gA)
        rstd_of(13)
        t4_gpsimd(gA)
        t2_gpsimd(gC)
        t4_gpsimd(gC)
        final(L - 8, bank0, 0)
        final(L - 7, bank0, G)
        bank1 = psy.tile([P, 2 * G * O], F32, name="yy")
        centre(L - 6, bank1, 0)
        centre(L - 5, bank1, G)
        vector_odd(A)
        stats(L - 3, own[L - 3])
        quantise_odd(gA)
        quantise_even(gA)
        evacuate(both(L - 1))
        nc.scalar.activation(out=warm[:], in_=eps[:], func=ACT.Abs_reciprocal_sqrt)
        own_bank(L - 1)
        parts = [scaled_by_scalar(L - 6, bank1, 0), scaled_by_scalar(L - 5, bank1, G)]
        biased_by_gpsimd(L - 6, parts[0])
        vector_odd(C)
        quantise_t1(both(L))
        quantise_odd(gC)
        quantise_even(gC)
        stats(L - 2, own[L - 2])
        add_eps(14)
        rstd_of(14)
        biased_by_gpsimd(L - 5, parts[1])
        mx(A, new_yt())
        mx(C, psz.tile([P, I], F32, name="zp"))
        evacuate(A)
        evacuate(C)
        stats(L - 1, own[L - 1])
        rstd_by_scalar(L - 1)
        final(L - 4, own[L - 4], G)
        own_bank(L)
        final(L - 3, own[L - 3], G)
        stats(L, own[L])
        final(L - 2, own[L - 2], G)
        rstd_by_scalar(L)
        final(L - 1, own[L - 1], G)
        final(L, own[L], G)
